import numpy as np
import ml_dtypes


def mxq(x, axis, fmt="e4m3"):
    dtype, down = {"e4m3": (ml_dtypes.float8_e4m3fn, 7), "e5m2": (ml_dtypes.float8_e5m2, 14)}[fmt]
    v = np.moveaxis(np.asarray(x, np.float32).astype(ml_dtypes.bfloat16).astype(np.float64), axis, -1)
    blocks = v.reshape(v.shape[:-1] + (-1, 32))
    amax = np.abs(blocks).max(-1, keepdims=True)
    byte = np.maximum(np.where(amax > 0, np.frexp(amax)[1] - 1 + 127, 0) - down, 1)
    scale = np.exp2(byte - 127.0)
    codes = (blocks / scale).astype(np.float32).astype(dtype).astype(np.float64)
    return np.moveaxis((codes * scale).reshape(v.shape), -1, axis)


WIDE = False


def mx_kscale(k):
    if not WIDE:
        return np.ones(k)
    levels = np.array([10, -10, 5, -5, 0])
    a = np.random.permutation(np.resize(levels, k // 512 * 4)).reshape(k // 512, 4)
    idx = np.arange(k)
    return np.exp2(a[idx // 512, idx % 128 // 32])


BF16 = ml_dtypes.bfloat16


def bf(x):
    return np.asarray(x, np.float32).astype(BF16)


def f64(x):
    return np.asarray(x).astype(np.float64)


B, L1, L2, D = 1, 1024, 512, 1024
NEG = -1e30


def setup_inputs():
    s = mx_kscale(D)
    return {"q": bf(np.random.standard_normal((B, L1, D)) * 1.4),
            "k": bf(np.random.standard_normal((B, L2, D)) * 1.4),
            "x1": bf(np.random.standard_normal((B, L1, D)) * s),
            "x2": bf(np.random.standard_normal((B, L2, D)) * s),
            "mask": bf(np.random.uniform(size=(B, L2)) > 0.1),
            "Wv": bf(np.random.standard_normal((D, D)) * 1.5 / np.sqrt(D) / s[None, :]),
            "bv": bf(np.random.standard_normal(D) * 0.5)}


def reference(q, k, x1, x2, mask, Wv, bv):
    m = f64(mask)
    wvq = mxq(f64(Wv), 1, "e4m3")
    v2 = (mxq(f64(x2), 2, "e4m3") @ wvq.T) + f64(bv)
    v1 = (mxq(f64(x1), 2, "e4m3") @ wvq.T) + f64(bv)
    a = f64(q) @ f64(k).transpose(0, 2, 1) * (1.0 / np.sqrt(D))
    a = a + (1.0 - m)[:, None, :] * NEG
    e2 = np.exp(a - a.max(2, keepdims=True))
    x2_out = (mxq(e2, 2, "e4m3") @ mxq(v2, 1, "e4m3")) / e2.sum(2, keepdims=True)
    e1 = np.exp(a - a.max(1, keepdims=True))
    x1_mid = (mxq(e1, 1, "e4m3").transpose(0, 2, 1) @ mxq(v1, 1, "e4m3")) / e1.sum(1)[:, :, None]
    x1_mid = x1_mid * m[:, :, None]
    return x2_out, x1_mid

@@ -1,0 +1,368 @@
+from contextlib import ExitStack
+
+import concourse.mybir as mybir
+from concourse.masks import make_identity
+
+F32 = mybir.dt.float32
+BF16 = mybir.dt.bfloat16
+U32 = mybir.dt.uint32
+U8 = mybir.dt.uint8
+FP8X4 = mybir.dt.float8_e4m3fn_x4
+ALU = mybir.AluOpType
+ACT = mybir.ActivationFunctionType
+AX = mybir.AxisListType
+
+P = 128
+FLOPS = 2 * (1024 + 512) * 1024 * 1024 + 3 * 2 * 1024 * 512 * 1024
+PIN = False
+
+
+def tile_coattention_pa_kernel(tc, q, k, x1, x2, mask, Wv, bv, out_0, out_1):
+    nc = tc.nc
+    with ExitStack() as ctx:
+        if PIN:
+            ctx.enter_context(tc.manual_schedule())
+        const = ctx.enter_context(tc.tile_pool(name="const", bufs=1))
+        raw = ctx.enter_context(tc.tile_pool(name="raw", bufs=1))
+        keep = ctx.enter_context(tc.tile_pool(name="keep", bufs=1))
+        xgp = ctx.enter_context(tc.tile_pool(name="xgp", bufs=6))
+        egp = ctx.enter_context(tc.tile_pool(name="egp", bufs=3))
+        vgp = ctx.enter_context(tc.tile_pool(name="vgp", bufs=3))
+        ost = ctx.enter_context(tc.tile_pool(name="ost", bufs=6))
+        pt = ctx.enter_context(tc.psum_pool(name="pt", bufs=4))
+        pm = ctx.enter_context(tc.psum_pool(name="pm", bufs=4))
+
+        ident_f = const.tile([P, P], F32, name="ident_f")
+        make_identity(nc, ident_f[:])
+        ident_b = const.tile([P, P], BF16, name="ident_b")
+        make_identity(nc, ident_b[:])
+        ones = const.tile([P, P], BF16, name="ones")
+        nc.vector.memset(ones[:], 1.0)
+        rows = const.tile([P, 1536], BF16, name="rows")
+        nc.vector.memset(rows[:], 0.0)
+        nc.scalar.dma_start(out=rows[0:1, 1024:1536], in_=mask)
+        nc.scalar.dma_start(out=rows[0:1, 0:1024], in_=bv.rearrange("(o n) -> o n", o=1))
+        mcol_b = const.tile([P, 4], BF16, name="mcol_b")
+        nc.scalar.dma_start(out=mcol_b[:], in_=mask.rearrange("b (r j) -> (b r) j", j=4))
+        bias_bc = const.tile([P, 1024], F32, name="bias_bc")
+        mterm = const.tile([P, 512], F32, name="mterm")
+        mcol = const.tile([P, 4], F32, name="mcol")
+        nrm = const.tile([P, 8], F32, name="nrm")
+        rsum = const.tile([P, 8], F32, name="rsum")
+        rrs = const.tile([P, 8], F32, name="rrs")
+        ncm = const.tile([P, 4], F32, name="ncm")
+        cs = const.tile([P, 8], F32, name="cs")
+        csum = const.tile([P, 4], F32, name="csum")
+        crec = const.tile([P, 4], F32, name="crec")
+        rc = const.tile([P, 4], F32, name="rc")
+
+        k_raw = raw.tile([P, 4096], BF16, name="k_raw")
+        q_raw = [raw.tile([P, 4096], BF16, name="q_raw%d" % g) for g in range(2)]
+        x2_raw = raw.tile([P, 4096], BF16, name="x2_raw")
+        w_raw = [raw.tile([P, 4096], BF16, name="w_raw%d" % g) for g in range(2)]
+        x1_raw = [raw.tile([P, 4096], BF16, name="x1_raw%d" % g) for g in range(2)]
+        k_d = k.rearrange("b (p t) d -> (b p) t d", t=4)
+        q_d = q.rearrange("b (g p t) d -> (b g) p t d", g=2, t=4)
+        x2_d = x2.rearrange("b (p t) d -> (b p) t d", t=4)
+        x1_d = x1.rearrange("b (g p t) d -> (b g) p t d", g=2, t=4)
+        w_d = Wv.rearrange("(c p) d -> p c d", p=P)
+        o0_d = out_0.rearrange("b (g p t) d -> (b g) p t d", g=2, t=4)
+        o1_d = out_1.rearrange("b (r j) d -> (b r) j d", j=4)
+        for t in range(4):
+            nc.sync.dma_start(out=k_raw[:, 1024 * t:1024 * (t + 1)], in_=k_d[:, t, :])
+        for g in range(2):
+            for t in range(4):
+                nc.sync.dma_start(out=q_raw[g][:, 1024 * t:1024 * (t + 1)], in_=q_d[g][:, t, :])
+        nc.sync.dma_start(out=x2_raw[:].rearrange("p (t d) -> p t d", t=4), in_=x2_d)
+        for g in range(2):
+            nc.sync.dma_start(out=w_raw[g][:].rearrange("p (c d) -> p c d", c=4), in_=w_d[:, 4 * g:4 * (g + 1), :])
+        for g in range(2):
+            nc.sync.dma_start(out=x1_raw[g][:].rearrange("p (t d) -> p t d", t=4), in_=x1_d[g])
+
+        kT = keep.tile([P, 2048], F32, name="kT")
+        kT_w = kT[:].rearrange("p (u c) -> p u c", u=4)
+        kT_b = kT[:].bitcast(BF16).rearrange("p (u c e) -> p u c e", u=4, e=2)
+        qT = [keep.tile([P, 512], F32, name="qT%d" % i) for i in range(8)]
+        a_sb = [keep.tile([P, 512], F32, name="a_sb%d" % i) for i in range(8)]
+        cmax = keep.tile([P, 512], F32, name="cmax")
+        e2 = [keep.tile([P, 512], BF16, name="e2_%d" % i) for i in range(8)]
+        e1T = [keep.tile([P, 1024], BF16, name="e1T%d" % j) for j in range(4)]
+        x1c = [keep.tile([P, 256], U32, name="x1c%d" % i, align_bytes=64) for i in range(8)]
+        x1s = [keep.tile([P, 256], U8, name="x1s%d" % i, align_bytes=64) for i in range(8)]
+        x2c = [keep.tile([P, 256], U32, name="x2c%d" % i, align_bytes=64) for i in range(4)]
+        x2s = [keep.tile([P, 256], U8, name="x2s%d" % i, align_bytes=64) for i in range(4)]
+        wc = [keep.tile([P, 256], U32, name="wc%d" % i, align_bytes=64) for i in range(8)]
+        ws = [keep.tile([P, 256], U8, name="ws%d" % i, align_bytes=64) for i in range(8)]
+        e2c = [keep.tile([P, 256], U32, name="e2c%d" % i, align_bytes=64) for i in range(4)]
+        e2s = [keep.tile([P, 256], U8, name="e2s%d" % i, align_bytes=64) for i in range(4)]
+        e1c = [keep.tile([P, 256], U32, name="e1c%d" % i, align_bytes=64) for i in range(4)]
+        e1s = [keep.tile([P, 256], U8, name="e1s%d" % i, align_bytes=64) for i in range(4)]
+        v1c = [keep.tile([P, 1024], U32, name="v1c%d" % i, align_bytes=64) for i in range(2)]
+        v1s = [keep.tile([P, 1024], U8, name="v1s%d" % i, align_bytes=64) for i in range(2)]
+        v2c = keep.tile([P, 1024], U32, name="v2c", align_bytes=64)
+        v2s = keep.tile([P, 1024], U8, name="v2s", align_bytes=64)
+
+        waiting = []
+
+        issued = [0]
+
+        def flush(leave):
+            for n in range(issued[0], len(waiting) - leave):
+                codes, scales, src = waiting[n]
+                nc.vector.quantize_mx(out=codes.bitcast(FP8X4), scales=scales, in_=src)
+            issued[0] = max(issued[0], len(waiting) - leave)
+
+        def word_job(raw_tile, t, finish):
+            box = []
+            words = raw_tile[:].bitcast(F32)
+
+            def step(s):
+                if s == 0:
+                    box.append(pt.tile([P, 512], F32, tag="t", name="wbank"))
+                nc.tensor.transpose(box[0][:, P * s:P * (s + 1)],
+                                    words[:, 512 * t + P * s:512 * t + P * (s + 1)], ident_f[:])
+                if s == 3:
+                    finish(box[0])
+            return [(step, s) for s in range(4)]
+
+        def copy_on(eng, out, in_):
+            if eng == "s":
+                nc.scalar.copy(out=out, in_=in_)
+            else:
+                nc.vector.tensor_copy(out=out, in_=in_)
+
+        def fin_k(j, eng):
+            def fin(bank):
+                copy_on(eng, kT_w[:, :, P * j:P * (j + 1)], bank[:].rearrange("p (u r) -> p u r", u=4))
+            return fin
+
+        def fin_q(i, eng, extra):
+            def fin(bank):
+                copy_on(eng, qT[i][:], bank[:])
+                if extra is not None:
+                    extra()
+            return fin
+
+        def fin_mx(codes, scales, eng, extra):
+            def fin(bank):
+                xg = xgp.tile([P, 1024], BF16, tag="xg", name="xg", align_bytes=64)
+                copy_on(eng, xg[:].bitcast(F32).rearrange("p (g r u) -> p g r u", g=2, u=2),
+                        bank[:].rearrange("p (g u r) -> p g r u", g=2, u=2))
+                flush(0)
+                waiting.append((codes[:], scales[:], xg[:]))
+                if extra is not None:
+                    extra()
+            return fin
+
+        def run(steps):
+            for fn, s in steps:
+                fn(s)
+
+        def a_tile(i, steps, first):
+            a_ps = pm.tile([P, 512], F32, tag="m", name="a_ps")
+            qb = qT[i][:].bitcast(BF16).rearrange("p (u r e) -> p u r e", u=4, e=2)
+            done = 0
+            for n in range(8):
+                u, e = n // 2, n % 2
+                nc.tensor.matmul(a_ps[:], lhsT=qb[:, u, :, e], rhs=kT_b[:, u, :, e],
+                                 start=(n == 0), stop=(n == 7))
+                if n >= first:
+                    run(steps[done:done + 2])
+                    done += 2
+            run(steps[done:])
+            nc.vector.scalar_tensor_tensor(out=a_sb[i][:], in0=a_ps[:], scalar=0.03125, in1=mterm[:],
+                                           op0=ALU.mult, op1=ALU.add)
+            nc.vector.tensor_reduce(out=nrm[:, i:i + 1], in_=a_sb[i][:], axis=AX.X, op=ALU.max, negate=True)
+            if i == 1:
+                nc.vector.tensor_max(cmax[:], a_sb[0][:], a_sb[1][:])
+            elif i > 1:
+                nc.vector.tensor_max(cmax[:], cmax[:], a_sb[i][:])
+            flush(0)
+
+        def e2_exp(i):
+            def go():
+                nc.scalar.activation(out=e2[i][:], in_=a_sb[i][:], func=ACT.Exp, bias=nrm[:, i:i + 1],
+                                     scale=1.0, accum_out=rsum[:, i:i + 1])
+            return go
+
+        def e2_T(pr):
+            bank = pt.tile([P, 1024], BF16, tag="t", name="e2bank")
+            for ii in range(2):
+                for j in range(4):
+                    s = 4 * ii + j
+                    nc.tensor.transpose(bank[:, P * s:P * (s + 1)], e2[2 * pr + ii][:, P * j:P * (j + 1)], ident_b[:])
+            eg = egp.tile([P, 1024], BF16, tag="eg", name="eg", align_bytes=64)
+            nc.scalar.copy(out=eg[:].rearrange("p (a c j) -> p a c j", a=2, j=4),
+                           in_=bank[:].rearrange("p (a j c) -> p a c j", a=2, j=4))
+            waiting.append((e2c[pr][:], e2s[pr][:], eg[:]))
+
+        def v_bank(xc, xs, base, c, vg):
+            ps = pm.tile([P, 512], F32, tag="m", name="v_ps")
+            for t in range(4):
+                for g in range(2):
+                    nc.tensor.matmul_mx(out=ps[:, P * t:P * (t + 1)],
+                                        lhsT=xc[base + t][:, P * g:P * (g + 1)].bitcast(FP8X4),
+                                        lhsT_scale=xs[base + t][:, P * g:P * (g + 1)],
+                                        rhs=wc[c][:, P * g:P * (g + 1)].bitcast(FP8X4),
+                                        rhs_scale=ws[c][:, P * g:P * (g + 1)],
+                                        start=(g == 0), stop=(g == 1))
+            cc = c % 4
+            nc.vector.tensor_tensor(out=vg[:].rearrange("p (w t) -> p w t", t=4)[:, P * cc:P * (cc + 1), :],
+                                    in0=ps[:].rearrange("p (t w) -> p w t", t=4),
+                                    in1=bias_bc[:, P * c:P * (c + 1)].unsqueeze(2).to_broadcast([P, P, 4]),
+                                    op=ALU.add)
+
+        def new_vg():
+            vg = vgp.tile([P, 2048], BF16, tag="vg", name="vg", align_bytes=64)
+            return vg
+
+        def scale_out(eng, o, ps, sc):
+            if eng == "s":
+                nc.scalar.activation(out=o[:], in_=ps[:], func=ACT.Copy, scale=sc)
+            else:
+                nc.vector.tensor_scalar_mul(out=o[:], in0=ps[:], scalar1=sc)
+
+        def x2o(i, h, eng):
+            ps = pm.tile([P, 512], F32, tag="m", name="o2_ps")
+            pr, ii = i // 2, i % 2
+            nc.tensor.matmul_mx(out=ps[:], lhsT=e2c[pr][:, P * ii:P * (ii + 1)].bitcast(FP8X4),
+                                lhsT_scale=e2s[pr][:, P * ii:P * (ii + 1)],
+                                rhs=v2c[:, 512 * h:512 * (h + 1)].bitcast(FP8X4),
+                                rhs_scale=v2s[:, 512 * h:512 * (h + 1)], start=True, stop=True)
+            o = ost.tile([P, 512], F32, tag="o", name="o")
+            scale_out(eng, o, ps, rrs[:, i:i + 1])
+            nc.sync.dma_start(out=o0_d[i // 4][:, i % 4, 512 * h:512 * (h + 1)], in_=o[:])
+
+        def x1m(j, h, eng):
+            ps = pm.tile([P, 512], F32, tag="m", name="o1_ps")
+            for g in range(2):
+                nc.tensor.matmul_mx(out=ps[:], lhsT=e1c[j][:, P * g:P * (g + 1)].bitcast(FP8X4),
+                                    lhsT_scale=e1s[j][:, P * g:P * (g + 1)],
+                                    rhs=v1c[g][:, 512 * h:512 * (h + 1)].bitcast(FP8X4),
+                                    rhs_scale=v1s[g][:, 512 * h:512 * (h + 1)], start=(g == 0), stop=(g == 1))
+            o = ost.tile([P, 512], F32, tag="o", name="o")
+            scale_out(eng, o, ps, rc[:, j:j + 1])
+            nc.sync.dma_start(out=o1_d[:, j, 512 * h:512 * (h + 1)], in_=o[:])
+
+        def colmax_T():
+            bank = pt.tile([P, 512], F32, tag="t", name="cbank")
+            for j in range(4):
+                nc.tensor.transpose(bank[:, P * j:P * (j + 1)], cmax[:, P * j:P * (j + 1)], ident_f[:])
+            nc.vector.tensor_reduce(out=ncm[:], in_=bank[:].rearrange("p (j c) -> p j c", j=4), axis=AX.X,
+                                    op=ALU.max, negate=True)
+
+        def a_T(j):
+            for hh in range(2):
+                bank = pt.tile([P, 512], F32, tag="t", name="aTbank")
+                for ii in range(4):
+                    nc.tensor.transpose(bank[:, P * ii:P * (ii + 1)], a_sb[4 * hh + ii][:, P * j:P * (j + 1)], ident_f[:])
+                nc.scalar.activation(out=e1T[j][:, 512 * hh:512 * (hh + 1)], in_=bank[:], func=ACT.Exp,
+                                     bias=ncm[:, j:j + 1], scale=1.0, accum_out=cs[:, 2 * j + hh:2 * j + hh + 1])
+
+        def e1_T(j):
+            bank = pt.tile([P, 1024], BF16, tag="t", name="e1bank")
+            for i in range(8):
+                nc.tensor.transpose(bank[:, P * i:P * (i + 1)], e1T[j][:, P * i:P * (i + 1)], ident_b[:])
+            eg = egp.tile([P, 1024], BF16, tag="eg", name="eg", align_bytes=64)
+            nc.scalar.copy(out=eg[:].rearrange("p (g r t) -> p g r t", g=2, t=4),
+                           in_=bank[:].rearrange("p (g t r) -> p g r t", g=2, t=4))
+            waiting.append((e1c[j][:], e1s[j][:], eg[:]))
+
+        for j in range(4):
+            run(word_job(k_raw, j, fin_k(j, "sv"[j % 2])))
+        run(word_job(q_raw[0], 0, fin_q(0, "s", None)))
+        m_ps = pm.tile([P, 512], F32, tag="m", name="m_ps")
+        nc.tensor.matmul(m_ps[:], lhsT=ones[:], rhs=rows[:, 1024:1536], start=True, stop=True)
+        nc.vector.tensor_scalar(out=mterm[:].rearrange("p (j r) -> p j r", j=4),
+                                in0=m_ps[:].rearrange("p (r j) -> p j r", j=4),
+                                scalar1=1.0e30, scalar2=-1.0e30, op0=ALU.mult, op1=ALU.add)
+        for h in range(2):
+            b_ps = pm.tile([P, 512], F32, tag="m", name="b_ps")
+            nc.tensor.matmul(b_ps[:], lhsT=ones[:], rhs=rows[:, 512 * h:512 * (h + 1)], start=True, stop=True)
+            nc.vector.tensor_copy(out=bias_bc[:, 512 * h:512 * (h + 1)], in_=b_ps[:])
+        nc.vector.tensor_copy(out=mcol[:], in_=mcol_b[:])
+
+        def qj(i, extra):
+            return word_job(q_raw[i // 4], i % 4, fin_q(i, "s", extra))
+
+        def x2j(i, extra):
+            return word_job(x2_raw, i, fin_mx(x2c[i], x2s[i], "s", extra))
+
+        def wj(i, extra):
+            return word_job(w_raw[i // 4], i % 4, fin_mx(wc[i], ws[i], "s", extra))
+
+        def x1j(i, extra):
+            return word_job(x1_raw[i // 4], i % 4, fin_mx(x1c[i], x1s[i], "s", extra))
+
+        a_tile(0, qj(1, None) + qj(2, None) + qj(3, None), 0)
+        a_tile(1, qj(4, None) + qj(5, e2_exp(0)) + qj(6, None) + qj(7, None), 0)
+        a_tile(2, x2j(0, e2_exp(1)) + x2j(1, None), 4)
+        a_tile(3, x2j(2, None) + x2j(3, e2_exp(2)) + wj(0, None) + wj(1, None), 0)
+        a_tile(4, wj(2, None) + wj(3, e2_exp(3)) + wj(4, None), 2)
+        a_tile(5, wj(5, None) + wj(6, e2_exp(4)) + wj(7, None), 0)
+        a_tile(6, x1j(0, None) + x1j(1, e2_exp(5)) + x1j(2, None) + x1j(3, None), 0)
+        a_tile(7, x1j(4, None) + x1j(5, e2_exp(6)) + x1j(6, None) + x1j(7, None), 0)
+        e2_exp(7)()
+
+        e2_T(0)
+        e2_T(1)
+        nc.vector.reciprocal(out=rrs[:], in_=rsum[:])
+        vg = new_vg()
+        for c in range(4):
+            v_bank(x2c, x2s, 0, c, vg)
+            if c == 1:
+                flush(0)
+        waiting.append((v2c[:, 0:512], v2s[:, 0:512], vg[:]))
+        e2_T(2)
+        e2_T(3)
+        colmax_T()
+        vg = new_vg()
+        for c in range(4, 8):
+            v_bank(x2c, x2s, 0, c, vg)
+            if c == 4:
+                flush(0)
+        waiting.append((v2c[:, 512:1024], v2s[:, 512:1024], vg[:]))
+        vg = new_vg()
+        for n in range(4):
+            x2o(2 * n, 0, "s")
+            x2o(2 * n + 1, 0, "s")
+            v_bank(x1c, x1s, 0, n, vg)
+            flush(0)
+        waiting.append((v1c[0][:, 0:512], v1s[0][:, 0:512], vg[:]))
+        a_T(0)
+        a_T(1)
+        vg = new_vg()
+        for n in range(4):
+            x2o(2 * n, 1, "s")
+            x2o(2 * n + 1, 1, "sv"[n % 2])
+            v_bank(x1c, x1s, 4, n, vg)
+            flush(0)
+        waiting.append((v1c[1][:, 0:512], v1s[1][:, 0:512], vg[:]))
+        e1_T(0)
+        e1_T(1)
+        a_T(2)
+        vg = new_vg()
+        for c in range(4, 8):
+            v_bank(x1c, x1s, 0, c, vg)
+            flush(0)
+        waiting.append((v1c[0][:, 512:1024], v1s[0][:, 512:1024], vg[:]))
+        a_T(3)
+        e1_T(2)
+        nc.vector.tensor_reduce(out=csum[:], in_=cs[:].rearrange("p (j h) -> p j h", h=2), axis=AX.X, op=ALU.add)
+        nc.vector.reciprocal(out=crec[:], in_=csum[:])
+        nc.vector.tensor_mul(rc[:], crec[:], mcol[:])
+        vg = new_vg()
+        for c in range(4, 6):
+            v_bank(x1c, x1s, 4, c, vg)
+            flush(0)
+        e1_T(3)
+        for c in range(6, 8):
+            v_bank(x1c, x1s, 4, c, vg)
+            flush(0)
+        waiting.append((v1c[1][:, 512:1024], v1s[1][:, 512:1024], vg[:]))
+        for j in range(4):
+            x1m(j, 0, "sv"[j % 2])
+            if j == 0:
+                flush(0)
+        for j in range(4):
+            x1m(j, 1, "sv"[j % 2])

@@ -14,7 +14,7 @@ AX = mybir.AxisListType
 
 P = 128
 FLOPS = 2 * (1024 + 512) * 1024 * 1024 + 3 * 2 * 1024 * 512 * 1024
-PIN = False
+PIN = True
 
 
 def tile_coattention_pa_kernel(tc, q, k, x1, x2, mask, Wv, bv, out_0, out_1):
@@ -306,7 +306,6 @@ def tile_coattention_pa_kernel(tc, q, k, x1, x2, mask, Wv, bv, out_0, out_1):
 
         e2_T(0)
         e2_T(1)
-        nc.vector.reciprocal(out=rrs[:], in_=rsum[:])
         vg = new_vg()
         for c in range(4):
             v_bank(x2c, x2s, 0, c, vg)
@@ -321,6 +320,7 @@ def tile_coattention_pa_kernel(tc, q, k, x1, x2, mask, Wv, bv, out_0, out_1):
             v_bank(x2c, x2s, 0, c, vg)
             if c == 4:
                 flush(0)
+                nc.vector.reciprocal(out=rrs[:], in_=rsum[:])
         waiting.append((v2c[:, 512:1024], v2s[:, 512:1024], vg[:]))
         vg = new_vg()
         for n in range(4):

@@ -14,23 +14,18 @@ AX = mybir.AxisListType
 
 P = 128
 FLOPS = 2 * (1024 + 512) * 1024 * 1024 + 3 * 2 * 1024 * 512 * 1024
-PIN = True
+SCALE = 0.03125
 
 
 def tile_coattention_pa_kernel(tc, q, k, x1, x2, mask, Wv, bv, out_0, out_1):
     nc = tc.nc
     with ExitStack() as ctx:
-        if PIN:
-            ctx.enter_context(tc.manual_schedule())
+        ctx.enter_context(tc.manual_schedule())
         const = ctx.enter_context(tc.tile_pool(name="const", bufs=1))
-        raw = ctx.enter_context(tc.tile_pool(name="raw", bufs=1))
         keep = ctx.enter_context(tc.tile_pool(name="keep", bufs=1))
-        xgp = ctx.enter_context(tc.tile_pool(name="xgp", bufs=6))
-        egp = ctx.enter_context(tc.tile_pool(name="egp", bufs=3))
+        egp = ctx.enter_context(tc.tile_pool(name="egp", bufs=4))
         vgp = ctx.enter_context(tc.tile_pool(name="vgp", bufs=3))
-        ost = ctx.enter_context(tc.tile_pool(name="ost", bufs=6))
-        pt = ctx.enter_context(tc.psum_pool(name="pt", bufs=4))
-        pm = ctx.enter_context(tc.psum_pool(name="pm", bufs=4))
+        ps = ctx.enter_context(tc.psum_pool(name="ps", bufs=8))
 
         ident_f = const.tile([P, P], F32, name="ident_f")
         make_identity(nc, ident_f[:])
@@ -38,53 +33,30 @@ def tile_coattention_pa_kernel(tc, q, k, x1, x2, mask, Wv, bv, out_0, out_1):
         make_identity(nc, ident_b[:])
         ones = const.tile([P, P], BF16, name="ones")
         nc.vector.memset(ones[:], 1.0)
-        rows = const.tile([P, 1536], BF16, name="rows")
+        rows = const.tile([P, 1024], BF16, name="rows")
         nc.vector.memset(rows[:], 0.0)
-        nc.scalar.dma_start(out=rows[0:1, 1024:1536], in_=mask)
-        nc.scalar.dma_start(out=rows[0:1, 0:1024], in_=bv.rearrange("(o n) -> o n", o=1))
         mcol_b = const.tile([P, 4], BF16, name="mcol_b")
         nc.scalar.dma_start(out=mcol_b[:], in_=mask.rearrange("b (r j) -> (b r) j", j=4))
+        nc.scalar.dma_start(out=rows[0:1, :], in_=bv.rearrange("(o n) -> o n", o=1))
         bias_bc = const.tile([P, 1024], F32, name="bias_bc")
-        mterm = const.tile([P, 512], F32, name="mterm")
         mcol = const.tile([P, 4], F32, name="mcol")
-        nrm = const.tile([P, 8], F32, name="nrm")
-        rsum = const.tile([P, 8], F32, name="rsum")
-        rrs = const.tile([P, 8], F32, name="rrs")
+        mterm = const.tile([P, 4], F32, name="mterm")
+        cmx = const.tile([P, 8], F32, name="cmx")
+        cm4 = const.tile([P, 4], F32, name="cm4")
         ncm = const.tile([P, 4], F32, name="ncm")
-        cs = const.tile([P, 8], F32, name="cs")
         csum = const.tile([P, 4], F32, name="csum")
         crec = const.tile([P, 4], F32, name="crec")
         rc = const.tile([P, 4], F32, name="rc")
+        rmx = const.tile([P, 8], F32, name="rmx")
+        nrm = const.tile([P, 8], F32, name="nrm")
+        rsum = const.tile([P, 8], F32, name="rsum")
+        rrs = const.tile([P, 8], F32, name="rrs")
 
-        k_raw = raw.tile([P, 4096], BF16, name="k_raw")
-        q_raw = [raw.tile([P, 4096], BF16, name="q_raw%d" % g) for g in range(2)]
-        x2_raw = raw.tile([P, 4096], BF16, name="x2_raw")
-        w_raw = [raw.tile([P, 4096], BF16, name="w_raw%d" % g) for g in range(2)]
-        x1_raw = [raw.tile([P, 4096], BF16, name="x1_raw%d" % g) for g in range(2)]
-        k_d = k.rearrange("b (p t) d -> (b p) t d", t=4)
-        q_d = q.rearrange("b (g p t) d -> (b g) p t d", g=2, t=4)
-        x2_d = x2.rearrange("b (p t) d -> (b p) t d", t=4)
-        x1_d = x1.rearrange("b (g p t) d -> (b g) p t d", g=2, t=4)
-        w_d = Wv.rearrange("(c p) d -> p c d", p=P)
         o0_d = out_0.rearrange("b (g p t) d -> (b g) p t d", g=2, t=4)
         o1_d = out_1.rearrange("b (r j) d -> (b r) j d", j=4)
-        for t in range(4):
-            nc.sync.dma_start(out=k_raw[:, 1024 * t:1024 * (t + 1)], in_=k_d[:, t, :])
-        for g in range(2):
-            for t in range(4):
-                nc.sync.dma_start(out=q_raw[g][:, 1024 * t:1024 * (t + 1)], in_=q_d[g][:, t, :])
-        nc.sync.dma_start(out=x2_raw[:].rearrange("p (t d) -> p t d", t=4), in_=x2_d)
-        for g in range(2):
-            nc.sync.dma_start(out=w_raw[g][:].rearrange("p (c d) -> p c d", c=4), in_=w_d[:, 4 * g:4 * (g + 1), :])
-        for g in range(2):
-            nc.sync.dma_start(out=x1_raw[g][:].rearrange("p (t d) -> p t d", t=4), in_=x1_d[g])
 
-        kT = keep.tile([P, 2048], F32, name="kT")
-        kT_w = kT[:].rearrange("p (u c) -> p u c", u=4)
-        kT_b = kT[:].bitcast(BF16).rearrange("p (u c e) -> p u c e", u=4, e=2)
-        qT = [keep.tile([P, 512], F32, name="qT%d" % i) for i in range(8)]
-        a_sb = [keep.tile([P, 512], F32, name="a_sb%d" % i) for i in range(8)]
-        cmax = keep.tile([P, 512], F32, name="cmax")
+        aT = [keep.tile([P, 1024], F32, name="aT%d" % j) for j in range(4)]
+        rm = [keep.tile([P, 512], F32, name="rm%d" % h) for h in range(2)]
         e2 = [keep.tile([P, 512], BF16, name="e2_%d" % i) for i in range(8)]
         e1T = [keep.tile([P, 1024], BF16, name="e1T%d" % j) for j in range(4)]
         x1c = [keep.tile([P, 256], U32, name="x1c%d" % i, align_bytes=64) for i in range(8)]
@@ -103,27 +75,13 @@ def tile_coattention_pa_kernel(tc, q, k, x1, x2, mask, Wv, bv, out_0, out_1):
         v2s = keep.tile([P, 1024], U8, name="v2s", align_bytes=64)
 
         waiting = []
-
         issued = [0]
 
-        def flush(leave):
-            for n in range(issued[0], len(waiting) - leave):
+        def flush():
+            for n in range(issued[0], len(waiting)):
                 codes, scales, src = waiting[n]
                 nc.vector.quantize_mx(out=codes.bitcast(FP8X4), scales=scales, in_=src)
-            issued[0] = max(issued[0], len(waiting) - leave)
-
-        def word_job(raw_tile, t, finish):
-            box = []
-            words = raw_tile[:].bitcast(F32)
-
-            def step(s):
-                if s == 0:
-                    box.append(pt.tile([P, 512], F32, tag="t", name="wbank"))
-                nc.tensor.transpose(box[0][:, P * s:P * (s + 1)],
-                                    words[:, 512 * t + P * s:512 * t + P * (s + 1)], ident_f[:])
-                if s == 3:
-                    finish(box[0])
-            return [(step, s) for s in range(4)]
+            issued[0] = len(waiting)
 
         def copy_on(eng, out, in_):
             if eng == "s":
@@ -131,76 +89,65 @@ def tile_coattention_pa_kernel(tc, q, k, x1, x2, mask, Wv, bv, out_0, out_1):
             else:
                 nc.vector.tensor_copy(out=out, in_=in_)
 
-        def fin_k(j, eng):
-            def fin(bank):
-                copy_on(eng, kT_w[:, :, P * j:P * (j + 1)], bank[:].rearrange("p (u r) -> p u r", u=4))
-            return fin
+        def job(count, dtype, ident, src_of, finish):
+            box = []
 
-        def fin_q(i, eng, extra):
-            def fin(bank):
-                copy_on(eng, qT[i][:], bank[:])
-                if extra is not None:
-                    extra()
-            return fin
+            def step(s):
+                if s == 0:
+                    box.append(ps.tile([P, count * P], dtype, tag="b", name="bank"))
+                nc.tensor.transpose(box[0][:, P * s:P * (s + 1)], src_of(s), ident[:])
+                if s == count - 1:
+                    finish(box[0])
+            return [(step, s) for s in range(count)]
 
-        def fin_mx(codes, scales, eng, extra):
-            def fin(bank):
-                xg = xgp.tile([P, 1024], BF16, tag="xg", name="xg", align_bytes=64)
-                copy_on(eng, xg[:].bitcast(F32).rearrange("p (g r u) -> p g r u", g=2, u=2),
-                        bank[:].rearrange("p (g u r) -> p g r u", g=2, u=2))
-                flush(0)
-                waiting.append((codes[:], scales[:], xg[:]))
-                if extra is not None:
-                    extra()
-            return fin
+        def rm_job(h):
+            def finish(bank):
+                nc.vector.tensor_reduce(out=rmx[:, 4 * h:4 * h + 4], in_=bank[:].rearrange("p (i r) -> p i r", i=4),
+                                        axis=AX.X, op=ALU.max)
+                nc.vector.tensor_scalar_mul(out=nrm[:, 4 * h:4 * h + 4], in0=rmx[:, 4 * h:4 * h + 4], scalar1=-SCALE)
+            return job(4, F32, ident_f, lambda s: rm[h][:, P * s:P * (s + 1)], finish)
+
+        def a_job(i):
+            def finish(bank):
+                nc.scalar.activation(out=e2[i][:], in_=bank[:], func=ACT.Exp, bias=nrm[:, i:i + 1], scale=SCALE,
+                                     accum_out=rsum[:, i:i + 1])
+            return job(4, F32, ident_f, lambda s: aT[s][:, P * i:P * (i + 1)], finish)
+
+        def e2_job(pr, eng):
+            def finish(bank):
+                eg = egp.tile([P, 1024], BF16, tag="eg", name="eg", align_bytes=64)
+                copy_on(eng, eg[:].rearrange("p (a c j) -> p a c j", a=2, j=4),
+                        bank[:].rearrange("p (a j c) -> p a c j", a=2, j=4))
+                flush()
+                nc.vector.reciprocal(out=rrs[:, 2 * pr:2 * pr + 2], in_=rsum[:, 2 * pr:2 * pr + 2])
+                waiting.append((e2c[pr][:], e2s[pr][:], eg[:]))
+            return job(8, BF16, ident_b, lambda s: e2[2 * pr + s // 4][:, P * (s % 4):P * (s % 4 + 1)], finish)
+
+        def e1_job(j, eng):
+            def finish(bank):
+                eg = egp.tile([P, 1024], BF16, tag="eg", name="eg", align_bytes=64)
+                copy_on(eng, eg[:].rearrange("p (g r t) -> p g r t", g=2, t=4),
+                        bank[:].rearrange("p (g t r) -> p g r t", g=2, t=4))
+                flush()
+                waiting.append((e1c[j][:], e1s[j][:], eg[:]))
+            return job(8, BF16, ident_b, lambda s: e1T[j][:, P * s:P * (s + 1)], finish)
 
         def run(steps):
             for fn, s in steps:
                 fn(s)
 
-        def a_tile(i, steps, first):
-            a_ps = pm.tile([P, 512], F32, tag="m", name="a_ps")
-            qb = qT[i][:].bitcast(BF16).rearrange("p (u r e) -> p u r e", u=4, e=2)
-            done = 0
-            for n in range(8):
-                u, e = n // 2, n % 2
-                nc.tensor.matmul(a_ps[:], lhsT=qb[:, u, :, e], rhs=kT_b[:, u, :, e],
-                                 start=(n == 0), stop=(n == 7))
-                if n >= first:
-                    run(steps[done:done + 2])
-                    done += 2
-            run(steps[done:])
-            nc.vector.scalar_tensor_tensor(out=a_sb[i][:], in0=a_ps[:], scalar=0.03125, in1=mterm[:],
-                                           op0=ALU.mult, op1=ALU.add)
-            nc.vector.tensor_reduce(out=nrm[:, i:i + 1], in_=a_sb[i][:], axis=AX.X, op=ALU.max, negate=True)
-            if i == 1:
-                nc.vector.tensor_max(cmax[:], a_sb[0][:], a_sb[1][:])
-            elif i > 1:
-                nc.vector.tensor_max(cmax[:], cmax[:], a_sb[i][:])
-            flush(0)
+        queue = []
+        taken = [0]
 
-        def e2_exp(i):
-            def go():
-                nc.scalar.activation(out=e2[i][:], in_=a_sb[i][:], func=ACT.Exp, bias=nrm[:, i:i + 1],
-                                     scale=1.0, accum_out=rsum[:, i:i + 1])
-            return go
-
-        def e2_T(pr):
-            bank = pt.tile([P, 1024], BF16, tag="t", name="e2bank")
-            for ii in range(2):
-                for j in range(4):
-                    s = 4 * ii + j
-                    nc.tensor.transpose(bank[:, P * s:P * (s + 1)], e2[2 * pr + ii][:, P * j:P * (j + 1)], ident_b[:])
-            eg = egp.tile([P, 1024], BF16, tag="eg", name="eg", align_bytes=64)
-            nc.scalar.copy(out=eg[:].rearrange("p (a c j) -> p a c j", a=2, j=4),
-                           in_=bank[:].rearrange("p (a j c) -> p a c j", a=2, j=4))
-            waiting.append((e2c[pr][:], e2s[pr][:], eg[:]))
+        def weave(n):
+            run(queue[taken[0]:taken[0] + n])
+            taken[0] = min(taken[0] + n, len(queue))
 
         def v_bank(xc, xs, base, c, vg):
-            ps = pm.tile([P, 512], F32, tag="m", name="v_ps")
+            acc = ps.tile([P, 512], F32, tag="b", name="v_ps")
             for t in range(4):
                 for g in range(2):
-                    nc.tensor.matmul_mx(out=ps[:, P * t:P * (t + 1)],
+                    nc.tensor.matmul_mx(out=acc[:, P * t:P * (t + 1)],
                                         lhsT=xc[base + t][:, P * g:P * (g + 1)].bitcast(FP8X4),
                                         lhsT_scale=xs[base + t][:, P * g:P * (g + 1)],
                                         rhs=wc[c][:, P * g:P * (g + 1)].bitcast(FP8X4),
@@ -208,161 +155,188 @@ def tile_coattention_pa_kernel(tc, q, k, x1, x2, mask, Wv, bv, out_0, out_1):
                                         start=(g == 0), stop=(g == 1))
             cc = c % 4
             nc.vector.tensor_tensor(out=vg[:].rearrange("p (w t) -> p w t", t=4)[:, P * cc:P * (cc + 1), :],
-                                    in0=ps[:].rearrange("p (t w) -> p w t", t=4),
+                                    in0=acc[:].rearrange("p (t w) -> p w t", t=4),
                                     in1=bias_bc[:, P * c:P * (c + 1)].unsqueeze(2).to_broadcast([P, P, 4]),
                                     op=ALU.add)
+            flush()
 
-        def new_vg():
+        def v_half(xc, xs, base, h, codes, scales, between):
             vg = vgp.tile([P, 2048], BF16, tag="vg", name="vg", align_bytes=64)
-            return vg
+            for cc in range(4):
+                v_bank(xc, xs, base, 4 * h + cc, vg)
+                between(cc)
+            waiting.append((codes[:, 512 * h:512 * (h + 1)], scales[:, 512 * h:512 * (h + 1)], vg[:]))
 
-        def scale_out(eng, o, ps, sc):
+        def scale_out(eng, acc, sc, dst):
+            o = ost.tile([P, 512], F32, tag="o", name="o")
             if eng == "s":
-                nc.scalar.activation(out=o[:], in_=ps[:], func=ACT.Copy, scale=sc)
+                nc.scalar.activation(out=o[:], in_=acc[:], func=ACT.Copy, scale=sc)
             else:
-                nc.vector.tensor_scalar_mul(out=o[:], in0=ps[:], scalar1=sc)
+                nc.vector.tensor_scalar_mul(out=o[:], in0=acc[:], scalar1=sc)
+            nc.sync.dma_start(out=dst, in_=o[:])
 
         def x2o(i, h, eng):
-            ps = pm.tile([P, 512], F32, tag="m", name="o2_ps")
+            acc = ps.tile([P, 512], F32, tag="b", name="o2_ps")
             pr, ii = i // 2, i % 2
-            nc.tensor.matmul_mx(out=ps[:], lhsT=e2c[pr][:, P * ii:P * (ii + 1)].bitcast(FP8X4),
+            nc.tensor.matmul_mx(out=acc[:], lhsT=e2c[pr][:, P * ii:P * (ii + 1)].bitcast(FP8X4),
                                 lhsT_scale=e2s[pr][:, P * ii:P * (ii + 1)],
                                 rhs=v2c[:, 512 * h:512 * (h + 1)].bitcast(FP8X4),
                                 rhs_scale=v2s[:, 512 * h:512 * (h + 1)], start=True, stop=True)
-            o = ost.tile([P, 512], F32, tag="o", name="o")
-            scale_out(eng, o, ps, rrs[:, i:i + 1])
-            nc.sync.dma_start(out=o0_d[i // 4][:, i % 4, 512 * h:512 * (h + 1)], in_=o[:])
+            scale_out(eng, acc, rrs[:, i:i + 1], o0_d[i // 4][:, i % 4, 512 * h:512 * (h + 1)])
 
         def x1m(j, h, eng):
-            ps = pm.tile([P, 512], F32, tag="m", name="o1_ps")
+            acc = ps.tile([P, 512], F32, tag="b", name="o1_ps")
             for g in range(2):
-                nc.tensor.matmul_mx(out=ps[:], lhsT=e1c[j][:, P * g:P * (g + 1)].bitcast(FP8X4),
+                nc.tensor.matmul_mx(out=acc[:], lhsT=e1c[j][:, P * g:P * (g + 1)].bitcast(FP8X4),
                                     lhsT_scale=e1s[j][:, P * g:P * (g + 1)],
                                     rhs=v1c[g][:, 512 * h:512 * (h + 1)].bitcast(FP8X4),
                                     rhs_scale=v1s[g][:, 512 * h:512 * (h + 1)], start=(g == 0), stop=(g == 1))
-            o = ost.tile([P, 512], F32, tag="o", name="o")
-            scale_out(eng, o, ps, rc[:, j:j + 1])
-            nc.sync.dma_start(out=o1_d[:, j, 512 * h:512 * (h + 1)], in_=o[:])
+            scale_out(eng, acc, rc[:, j:j + 1], o1_d[:, j, 512 * h:512 * (h + 1)])
 
-        def colmax_T():
-            bank = pt.tile([P, 512], F32, tag="t", name="cbank")
-            for j in range(4):
-                nc.tensor.transpose(bank[:, P * j:P * (j + 1)], cmax[:, P * j:P * (j + 1)], ident_f[:])
-            nc.vector.tensor_reduce(out=ncm[:], in_=bank[:].rearrange("p (j c) -> p j c", j=4), axis=AX.X,
-                                    op=ALU.max, negate=True)
-
-        def a_T(j):
-            for hh in range(2):
-                bank = pt.tile([P, 512], F32, tag="t", name="aTbank")
-                for ii in range(4):
-                    nc.tensor.transpose(bank[:, P * ii:P * (ii + 1)], a_sb[4 * hh + ii][:, P * j:P * (j + 1)], ident_f[:])
-                nc.scalar.activation(out=e1T[j][:, 512 * hh:512 * (hh + 1)], in_=bank[:], func=ACT.Exp,
-                                     bias=ncm[:, j:j + 1], scale=1.0, accum_out=cs[:, 2 * j + hh:2 * j + hh + 1])
-
-        def e1_T(j):
-            bank = pt.tile([P, 1024], BF16, tag="t", name="e1bank")
-            for i in range(8):
-                nc.tensor.transpose(bank[:, P * i:P * (i + 1)], e1T[j][:, P * i:P * (i + 1)], ident_b[:])
-            eg = egp.tile([P, 1024], BF16, tag="eg", name="eg", align_bytes=64)
-            nc.scalar.copy(out=eg[:].rearrange("p (g r t) -> p g r t", g=2, t=4),
-                           in_=bank[:].rearrange("p (g t r) -> p g r t", g=2, t=4))
-            waiting.append((e1c[j][:], e1s[j][:], eg[:]))
-
-        for j in range(4):
-            run(word_job(k_raw, j, fin_k(j, "sv"[j % 2])))
-        run(word_job(q_raw[0], 0, fin_q(0, "s", None)))
-        m_ps = pm.tile([P, 512], F32, tag="m", name="m_ps")
-        nc.tensor.matmul(m_ps[:], lhsT=ones[:], rhs=rows[:, 1024:1536], start=True, stop=True)
-        nc.vector.tensor_scalar(out=mterm[:].rearrange("p (j r) -> p j r", j=4),
-                                in0=m_ps[:].rearrange("p (r j) -> p j r", j=4),
-                                scalar1=1.0e30, scalar2=-1.0e30, op0=ALU.mult, op1=ALU.add)
-        for h in range(2):
-            b_ps = pm.tile([P, 512], F32, tag="m", name="b_ps")
-            nc.tensor.matmul(b_ps[:], lhsT=ones[:], rhs=rows[:, 512 * h:512 * (h + 1)], start=True, stop=True)
-            nc.vector.tensor_copy(out=bias_bc[:, 512 * h:512 * (h + 1)], in_=b_ps[:])
         nc.vector.tensor_copy(out=mcol[:], in_=mcol_b[:])
+        nc.vector.tensor_scalar(out=mterm[:], in0=mcol[:], scalar1=1.0e30 / SCALE, scalar2=-1.0e30 / SCALE,
+                                op0=ALU.mult, op1=ALU.add)
 
-        def qj(i, extra):
-            return word_job(q_raw[i // 4], i % 4, fin_q(i, "s", extra))
+        with ExitStack() as early:
+            xgp = early.enter_context(tc.tile_pool(name="xgp", bufs=6))
+            raw = early.enter_context(tc.tile_pool(name="raw", bufs=1))
+            k_raw = raw.tile([P, 4096], BF16, name="k_raw")
+            q_raw = [raw.tile([P, 4096], BF16, name="q_raw%d" % g) for g in range(2)]
+            x2_raw = raw.tile([P, 4096], BF16, name="x2_raw")
+            w_raw = [raw.tile([P, 4096], BF16, name="w_raw%d" % g) for g in range(2)]
+            x1_raw = [raw.tile([P, 4096], BF16, name="x1_raw%d" % g) for g in range(2)]
+            k_d = k.rearrange("b (p t) d -> (b p) t d", t=4)
+            q_d = q.rearrange("b (g p t) d -> (b g) p t d", g=2, t=4)
+            x2_d = x2.rearrange("b (p t) d -> (b p) t d", t=4)
+            x1_d = x1.rearrange("b (g p t) d -> (b g) p t d", g=2, t=4)
+            w_d = Wv.rearrange("(c p) d -> p c d", p=P)
 
-        def x2j(i, extra):
-            return word_job(x2_raw, i, fin_mx(x2c[i], x2s[i], "s", extra))
+            def load(dst, t, src):
+                nc.sync.dma_start(out=dst[:, 1024 * t:1024 * (t + 1)], in_=src)
 
-        def wj(i, extra):
-            return word_job(w_raw[i // 4], i % 4, fin_mx(wc[i], ws[i], "s", extra))
+            load(k_raw, 0, k_d[:, 0, :])
+            for t in range(4):
+                load(q_raw[0], t, q_d[0][:, t, :])
+            for t in range(1, 4):
+                load(k_raw, t, k_d[:, t, :])
+            for t in range(4):
+                load(q_raw[1], t, q_d[1][:, t, :])
+            for t in range(4):
+                load(x2_raw, t, x2_d[:, t, :])
+            for c in range(8):
+                load(w_raw[c // 4], c % 4, w_d[:, c, :])
+            for i in range(8):
+                load(x1_raw[i // 4], i % 4, x1_d[i // 4][:, i % 4, :])
 
-        def x1j(i, extra):
-            return word_job(x1_raw[i // 4], i % 4, fin_mx(x1c[i], x1s[i], "s", extra))
+            kT = [raw.tile([P, 512], F32, name="kT%d" % j) for j in range(4)]
+            kT_b = [t[:].bitcast(BF16).rearrange("p (u r e) -> p u r e", u=4, e=2) for t in kT]
+            qT = [raw.tile([P, 2048], F32, name="qT%d" % h) for h in range(2)]
+            qT_w = [t[:].rearrange("p (u c) -> p u c", u=4) for t in qT]
+            qT_b = [t[:].bitcast(BF16).rearrange("p (u c e) -> p u c e", u=4, e=2) for t in qT]
 
-        a_tile(0, qj(1, None) + qj(2, None) + qj(3, None), 0)
-        a_tile(1, qj(4, None) + qj(5, e2_exp(0)) + qj(6, None) + qj(7, None), 0)
-        a_tile(2, x2j(0, e2_exp(1)) + x2j(1, None), 4)
-        a_tile(3, x2j(2, None) + x2j(3, e2_exp(2)) + wj(0, None) + wj(1, None), 0)
-        a_tile(4, wj(2, None) + wj(3, e2_exp(3)) + wj(4, None), 2)
-        a_tile(5, wj(5, None) + wj(6, e2_exp(4)) + wj(7, None), 0)
-        a_tile(6, x1j(0, None) + x1j(1, e2_exp(5)) + x1j(2, None) + x1j(3, None), 0)
-        a_tile(7, x1j(4, None) + x1j(5, e2_exp(6)) + x1j(6, None) + x1j(7, None), 0)
-        e2_exp(7)()
+            def words_of(raw_tile, t):
+                words = raw_tile[:].bitcast(F32)
+                return lambda s: words[:, 512 * t + P * s:512 * t + P * (s + 1)]
 
-        e2_T(0)
-        e2_T(1)
-        vg = new_vg()
-        for c in range(4):
-            v_bank(x2c, x2s, 0, c, vg)
-            if c == 1:
-                flush(0)
-        waiting.append((v2c[:, 0:512], v2s[:, 0:512], vg[:]))
-        e2_T(2)
-        e2_T(3)
-        colmax_T()
-        vg = new_vg()
-        for c in range(4, 8):
-            v_bank(x2c, x2s, 0, c, vg)
-            if c == 4:
-                flush(0)
-                nc.vector.reciprocal(out=rrs[:], in_=rsum[:])
-        waiting.append((v2c[:, 512:1024], v2s[:, 512:1024], vg[:]))
-        vg = new_vg()
-        for n in range(4):
-            x2o(2 * n, 0, "s")
-            x2o(2 * n + 1, 0, "s")
-            v_bank(x1c, x1s, 0, n, vg)
-            flush(0)
-        waiting.append((v1c[0][:, 0:512], v1s[0][:, 0:512], vg[:]))
-        a_T(0)
-        a_T(1)
-        vg = new_vg()
-        for n in range(4):
-            x2o(2 * n, 1, "s")
-            x2o(2 * n + 1, 1, "sv"[n % 2])
-            v_bank(x1c, x1s, 4, n, vg)
-            flush(0)
-        waiting.append((v1c[1][:, 0:512], v1s[1][:, 0:512], vg[:]))
-        e1_T(0)
-        e1_T(1)
-        a_T(2)
-        vg = new_vg()
-        for c in range(4, 8):
-            v_bank(x1c, x1s, 0, c, vg)
-            flush(0)
-        waiting.append((v1c[0][:, 512:1024], v1s[0][:, 512:1024], vg[:]))
-        a_T(3)
-        e1_T(2)
-        nc.vector.tensor_reduce(out=csum[:], in_=cs[:].rearrange("p (j h) -> p j h", h=2), axis=AX.X, op=ALU.add)
+            def k_job(j, eng):
+                return job(4, F32, ident_f, words_of(k_raw, j), lambda bank: copy_on(eng, kT[j][:], bank[:]))
+
+            def q_job(i, eng):
+                return job(4, F32, ident_f, words_of(q_raw[i // 4], i % 4),
+                           lambda bank: copy_on(eng, qT_w[i // 4][:, :, P * (i % 4):P * (i % 4 + 1)],
+                                                bank[:].rearrange("p (u r) -> p u r", u=4)))
+
+            def mx_job(raw_tile, t, codes, scales, eng):
+                def finish(bank):
+                    xg = xgp.tile([P, 1024], BF16, tag="xg", name="xg", align_bytes=64)
+                    copy_on(eng, xg[:].bitcast(F32).rearrange("p (g r u) -> p g r u", g=2, u=2),
+                            bank[:].rearrange("p (g u r) -> p g r u", g=2, u=2))
+                    flush()
+                    waiting.append((codes[:], scales[:], xg[:]))
+                return job(4, F32, ident_f, words_of(raw_tile, t), finish)
+
+            def leave_scores(acc, j, h):
+                half = aT[j][:, 512 * h:512 * (h + 1)]
+                nc.vector.tensor_scalar(out=half, in0=acc[:], scalar1=mterm[:, j:j + 1], scalar2=None, op0=ALU.add,
+                                        op1=ALU.max, accum_out=cmx[:, 4 * h + j:4 * h + j + 1])
+                if j == 1:
+                    nc.vector.tensor_max(rm[h][:], aT[0][:, 512 * h:512 * (h + 1)], half)
+                elif j > 1:
+                    nc.vector.tensor_max(rm[h][:], rm[h][:], half)
+
+            def score_pass(acc, j, h, cols, n):
+                nc.tensor.matmul(acc[:, cols], lhsT=kT_b[j][:, n // 2, :, n % 2], rhs=qT_b[h][:, n // 2, cols, n % 2],
+                                 start=(n == 0), stop=(n == 7))
+
+            run(k_job(0, "s"))
+            run(q_job(0, "v"))
+            acc = ps.tile([P, 512], F32, tag="b", name="acc")
+            for i in range(4):
+                if i < 3:
+                    run(q_job(i + 1, "sv"[i % 2]))
+                else:
+                    run(k_job(1, "s"))
+                for n in range(8):
+                    score_pass(acc, 0, 0, slice(P * i, P * (i + 1)), n)
+            leave_scores(acc, 0, 0)
+
+            for j in range(2, 4):
+                queue.extend(k_job(j, "s"))
+            for i in range(4, 8):
+                queue.extend(q_job(i, "ss"[i % 2]))
+            for i in range(4):
+                queue.extend(mx_job(x2_raw, i, x2c[i], x2s[i], "ssss"[i % 4]))
+            for c in range(8):
+                queue.extend(mx_job(w_raw[c // 4], c % 4, wc[c], ws[c], "ssss"[c % 4]))
+            for h in range(2):
+                for j in range(4):
+                    if (j, h) == (0, 0):
+                        continue
+                    if (j, h) == (1, 0):
+                        for hh in range(2):
+                            b_ps = ps.tile([P, 512], F32, tag="b", name="b_ps")
+                            nc.tensor.matmul(b_ps[:], lhsT=ones[:], rhs=rows[:, 512 * hh:512 * (hh + 1)], start=True, stop=True)
+                            weave(2)
+                            nc.vector.tensor_copy(out=bias_bc[:, 512 * hh:512 * (hh + 1)], in_=b_ps[:])
+                    if (j, h) == (1, 1):
+                        queue[taken[0]:taken[0]] = (rm_job(0) + a_job(0) + a_job(1) + a_job(2) + a_job(3)
+                                                    + e2_job(0, "s") + e2_job(1, "s"))
+                        for i in range(8):
+                            queue.extend(mx_job(x1_raw[i // 4], i % 4, x1c[i], x1s[i], "ssss"[i % 4]))
+                    acc = ps.tile([P, 512], F32, tag="b", name="acc")
+                    for n in range(8):
+                        score_pass(acc, j, h, slice(0, 512), n)
+                        weave(2)
+                    leave_scores(acc, j, h)
+
+            weave(len(queue))
+            nc.vector.tensor_reduce(out=cm4[:], in_=cmx[:].rearrange("p (h j) -> p j h", h=2), axis=AX.X, op=ALU.max)
+            nc.vector.tensor_scalar_mul(out=ncm[:], in0=cm4[:], scalar1=-SCALE)
+            run(rm_job(1) + a_job(4) + a_job(5) + a_job(6) + a_job(7))
+            flush()
+
+
+        ost = ctx.enter_context(tc.tile_pool(name="ost", bufs=16))
+        for j in range(4):
+            nc.scalar.activation(out=e1T[j][:], in_=aT[j][:], func=ACT.Exp, bias=ncm[:, j:j + 1], scale=SCALE,
+                                 accum_out=csum[:, j:j + 1])
+        for h in range(2):
+            v_half(x2c, x2s, 0, h, v2c, v2s, lambda cc: None)
+
+        def two_x2o(first, cc):
+            for i in range(2):
+                x2o(first + 2 * (cc % 2) + i, cc // 2, "ss"[(2 * cc + i) % 2])
+
+        run(e2_job(2, "s") + e2_job(3, "v"))
+        v_half(x1c, x1s, 0, 0, v1c[0], v1s[0], lambda cc: two_x2o(0, cc))
+        run(e1_job(0, "s") + e1_job(1, "v") + e1_job(2, "s") + e1_job(3, "v"))
         nc.vector.reciprocal(out=crec[:], in_=csum[:])
         nc.vector.tensor_mul(rc[:], crec[:], mcol[:])
-        vg = new_vg()
-        for c in range(4, 6):
-            v_bank(x1c, x1s, 4, c, vg)
-            flush(0)
-        e1_T(3)
-        for c in range(6, 8):
-            v_bank(x1c, x1s, 4, c, vg)
-            flush(0)
-        waiting.append((v1c[1][:, 512:1024], v1s[1][:, 512:1024], vg[:]))
-        for j in range(4):
+        v_half(x1c, x1s, 4, 0, v1c[1], v1s[1], lambda cc: two_x2o(4, cc))
+        v_half(x1c, x1s, 0, 1, v1c[0], v1s[0], lambda cc: None)
+        v_half(x1c, x1s, 4, 1, v1c[1], v1s[1], lambda cc: x1m(cc // 2, 0, "s") if cc % 2 == 1 else None)
+        for j in range(2, 4):
             x1m(j, 0, "sv"[j % 2])
-            if j == 0:
-                flush(0)
+            flush()
         for j in range(4):
             x1m(j, 1, "sv"[j % 2])

@@ -109,6 +109,8 @@ def tile_coattention_pa_kernel(tc, q, k, x1, x2, mask, Wv, bv, out_0, out_1):
 
         def a_job(i):
             def finish(bank):
+                nc.vector.tensor_reduce(out=rmx[:, i:i + 1], in_=bank[:], axis=AX.X, op=ALU.max)
+                nc.vector.tensor_scalar_mul(out=nrm[:, i:i + 1], in0=rmx[:, i:i + 1], scalar1=-SCALE)
                 nc.scalar.activation(out=e2[i][:], in_=bank[:], func=ACT.Exp, bias=nrm[:, i:i + 1], scale=SCALE,
                                      accum_out=rsum[:, i:i + 1])
             return job(4, F32, ident_f, lambda s: aT[s][:, P * i:P * (i + 1)], finish)
@@ -221,12 +223,16 @@ def tile_coattention_pa_kernel(tc, q, k, x1, x2, mask, Wv, bv, out_0, out_1):
                 load(k_raw, t, k_d[:, t, :])
             for t in range(4):
                 load(q_raw[1], t, q_d[1][:, t, :])
-            for t in range(4):
-                load(x2_raw, t, x2_d[:, t, :])
-            for c in range(8):
-                load(w_raw[c // 4], c % 4, w_d[:, c, :])
-            for i in range(8):
-                load(x1_raw[i // 4], i % 4, x1_d[i // 4][:, i % 4, :])
+
+            def load_two(dst, t, src):
+                nc.sync.dma_start(out=dst[:, 1024 * t:1024 * (t + 2)].rearrange("p (t d) -> p t d", t=2), in_=src)
+
+            for t in range(0, 4, 2):
+                load_two(x2_raw, t, x2_d[:, t:t + 2, :])
+            for c in range(0, 8, 2):
+                load_two(w_raw[c // 4], c % 4, w_d[:, c:c + 2, :])
+            for i in range(0, 8, 2):
+                load_two(x1_raw[i // 4], i % 4, x1_d[i // 4][:, i % 4:i % 4 + 2, :])
 
             kT = [raw.tile([P, 512], F32, name="kT%d" % j) for j in range(4)]
             kT_b = [t[:].bitcast(BF16).rearrange("p (u r e) -> p u r e", u=4, e=2) for t in kT]
@@ -259,10 +265,6 @@ def tile_coattention_pa_kernel(tc, q, k, x1, x2, mask, Wv, bv, out_0, out_1):
                 half = aT[j][:, 512 * h:512 * (h + 1)]
                 nc.vector.tensor_scalar(out=half, in0=acc[:], scalar1=mterm[:, j:j + 1], scalar2=None, op0=ALU.add,
                                         op1=ALU.max, accum_out=cmx[:, 4 * h + j:4 * h + j + 1])
-                if j == 1:
-                    nc.vector.tensor_max(rm[h][:], aT[0][:, 512 * h:512 * (h + 1)], half)
-                elif j > 1:
-                    nc.vector.tensor_max(rm[h][:], rm[h][:], half)
 
             def score_pass(acc, j, h, cols, n):
                 nc.tensor.matmul(acc[:, cols], lhsT=kT_b[j][:, n // 2, :, n % 2], rhs=qT_b[h][:, n // 2, cols, n % 2],
@@ -299,7 +301,7 @@ def tile_coattention_pa_kernel(tc, q, k, x1, x2, mask, Wv, bv, out_0, out_1):
                             weave(2)
                             nc.vector.tensor_copy(out=bias_bc[:, 512 * hh:512 * (hh + 1)], in_=b_ps[:])
                     if (j, h) == (1, 1):
-                        queue[taken[0]:taken[0]] = (rm_job(0) + a_job(0) + a_job(1) + a_job(2) + a_job(3)
+                        queue[taken[0]:taken[0]] = (a_job(0) + a_job(1) + a_job(2) + a_job(3)
                                                     + e2_job(0, "s") + e2_job(1, "s"))
                         for i in range(8):
                             queue.extend(mx_job(x1_raw[i // 4], i % 4, x1c[i], x1s[i], "ssss"[i % 4]))
@@ -312,22 +314,25 @@ def tile_coattention_pa_kernel(tc, q, k, x1, x2, mask, Wv, bv, out_0, out_1):
             weave(len(queue))
             nc.vector.tensor_reduce(out=cm4[:], in_=cmx[:].rearrange("p (h j) -> p j h", h=2), axis=AX.X, op=ALU.max)
             nc.vector.tensor_scalar_mul(out=ncm[:], in0=cm4[:], scalar1=-SCALE)
-            run(rm_job(1) + a_job(4) + a_job(5) + a_job(6) + a_job(7))
+            run(a_job(4) + a_job(5) + a_job(6) + a_job(7))
             flush()
 
+            def e1_exp(j):
+                nc.scalar.activation(out=e1T[j][:], in_=aT[j][:], func=ACT.Exp, bias=ncm[:, j:j + 1], scale=SCALE,
+                                     accum_out=csum[:, j:j + 1])
+
+            for j in range(4):
+                e1_exp(j)
+            for h in range(2):
+                v_half(x2c, x2s, 0, h, v2c, v2s, lambda cc: None)
+            run(e2_job(2, "s") + e2_job(3, "v"))
 
         ost = ctx.enter_context(tc.tile_pool(name="ost", bufs=16))
-        for j in range(4):
-            nc.scalar.activation(out=e1T[j][:], in_=aT[j][:], func=ACT.Exp, bias=ncm[:, j:j + 1], scale=SCALE,
-                                 accum_out=csum[:, j:j + 1])
-        for h in range(2):
-            v_half(x2c, x2s, 0, h, v2c, v2s, lambda cc: None)
 
         def two_x2o(first, cc):
             for i in range(2):
                 x2o(first + 2 * (cc % 2) + i, cc // 2, "ss"[(2 * cc + i) % 2])
 
-        run(e2_job(2, "s") + e2_job(3, "v"))
         v_half(x1c, x1s, 0, 0, v1c[0], v1s[0], lambda cc: two_x2o(0, cc))
         run(e1_job(0, "s") + e1_job(1, "v") + e1_job(2, "s") + e1_job(3, "v"))
         nc.vector.reciprocal(out=crec[:], in_=csum[:])

@@ -35,6 +35,9 @@ def tile_coattention_pa_kernel(tc, q, k, x1, x2, mask, Wv, bv, out_0, out_1):
         nc.vector.memset(ones[:], 1.0)
         rows = const.tile([P, 1024], BF16, name="rows")
         nc.vector.memset(rows[:], 0.0)
+        warm = const.tile([P, 2], F32, name="warm")
+        nc.vector.memset(warm[:], 0.0)
+        nc.scalar.activation(out=warm[:, 1:2], in_=warm[:, 0:1], func=ACT.Exp)
         mcol_b = const.tile([P, 4], BF16, name="mcol_b")
         nc.scalar.dma_start(out=mcol_b[:], in_=mask.rearrange("b (r j) -> (b r) j", j=4))
         nc.scalar.dma_start(out=rows[0:1, :], in_=bv.rearrange("(o n) -> o n", o=1))
@@ -195,9 +198,6 @@ def tile_coattention_pa_kernel(tc, q, k, x1, x2, mask, Wv, bv, out_0, out_1):
                                     rhs_scale=v1s[g][:, 512 * h:512 * (h + 1)], start=(g == 0), stop=(g == 1))
             scale_out(eng, acc, rc[:, j:j + 1], o1_d[:, j, 512 * h:512 * (h + 1)])
 
-        nc.vector.tensor_copy(out=mcol[:], in_=mcol_b[:])
-        nc.vector.tensor_scalar(out=mterm[:], in0=mcol[:], scalar1=1.0e30 / SCALE, scalar2=-1.0e30 / SCALE,
-                                op0=ALU.mult, op1=ALU.add)
 
         with ExitStack() as early:
             xgp = early.enter_context(tc.tile_pool(name="xgp", bufs=6))
@@ -280,6 +280,9 @@ def tile_coattention_pa_kernel(tc, q, k, x1, x2, mask, Wv, bv, out_0, out_1):
                     run(k_job(1, "s"))
                 for n in range(8):
                     score_pass(acc, 0, 0, slice(P * i, P * (i + 1)), n)
+            nc.vector.tensor_copy(out=mcol[:], in_=mcol_b[:])
+            nc.vector.tensor_scalar(out=mterm[:], in0=mcol[:], scalar1=1.0e30 / SCALE, scalar2=-1.0e30 / SCALE,
+                                    op0=ALU.mult, op1=ALU.add)
             leave_scores(acc, 0, 0)
 
             for j in range(2, 4):

@@ -29,8 +29,6 @@ def tile_coattention_pa_kernel(tc, q, k, x1, x2, mask, Wv, bv, out_0, out_1):
 
         ident_f = const.tile([P, P], F32, name="ident_f")
         make_identity(nc, ident_f[:])
-        ident_b = const.tile([P, P], BF16, name="ident_b")
-        make_identity(nc, ident_b[:])
         ones = const.tile([P, P], BF16, name="ones")
         nc.vector.memset(ones[:], 1.0)
         rows = const.tile([P, 1024], BF16, name="rows")
@@ -114,28 +112,29 @@ def tile_coattention_pa_kernel(tc, q, k, x1, x2, mask, Wv, bv, out_0, out_1):
             def finish(bank):
                 nc.vector.tensor_reduce(out=rmx[:, i:i + 1], in_=bank[:], axis=AX.X, op=ALU.max)
                 nc.vector.tensor_scalar_mul(out=nrm[:, i:i + 1], in0=rmx[:, i:i + 1], scalar1=-SCALE)
-                nc.scalar.activation(out=e2[i][:], in_=bank[:], func=ACT.Exp, bias=nrm[:, i:i + 1], scale=SCALE,
-                                     accum_out=rsum[:, i:i + 1])
+                nc.scalar.activation(out=e2[i][:].rearrange("p (u r e) -> p u r e", u=2, e=2),
+                                     in_=bank[:].rearrange("p (u e r) -> p u r e", u=2, e=2), func=ACT.Exp,
+                                     bias=nrm[:, i:i + 1], scale=SCALE, accum_out=rsum[:, i:i + 1])
             return job(4, F32, ident_f, lambda s: aT[s][:, P * i:P * (i + 1)], finish)
 
         def e2_job(pr, eng):
             def finish(bank):
                 eg = egp.tile([P, 1024], BF16, tag="eg", name="eg", align_bytes=64)
-                copy_on(eng, eg[:].rearrange("p (a c j) -> p a c j", a=2, j=4),
-                        bank[:].rearrange("p (a j c) -> p a c j", a=2, j=4))
+                copy_on(eng, eg[:].bitcast(F32).rearrange("p (a c u) -> p a c u", a=2, u=2),
+                        bank[:].rearrange("p (a u c) -> p a c u", a=2, u=2))
                 flush()
                 nc.vector.reciprocal(out=rrs[:, 2 * pr:2 * pr + 2], in_=rsum[:, 2 * pr:2 * pr + 2])
                 waiting.append((e2c[pr][:], e2s[pr][:], eg[:]))
-            return job(8, BF16, ident_b, lambda s: e2[2 * pr + s // 4][:, P * (s % 4):P * (s % 4 + 1)], finish)
+            return job(4, F32, ident_f, lambda s: e2[2 * pr + s // 2][:].bitcast(F32)[:, P * (s % 2):P * (s % 2 + 1)], finish)
 
         def e1_job(j, eng):
             def finish(bank):
                 eg = egp.tile([P, 1024], BF16, tag="eg", name="eg", align_bytes=64)
-                copy_on(eng, eg[:].rearrange("p (g r t) -> p g r t", g=2, t=4),
-                        bank[:].rearrange("p (g t r) -> p g r t", g=2, t=4))
+                copy_on(eng, eg[:].bitcast(F32).rearrange("p (g c u) -> p g c u", g=2, u=2),
+                        bank[:].rearrange("p (g u c) -> p g c u", g=2, u=2))
                 flush()
                 waiting.append((e1c[j][:], e1s[j][:], eg[:]))
-            return job(8, BF16, ident_b, lambda s: e1T[j][:, P * s:P * (s + 1)], finish)
+            return job(4, F32, ident_f, lambda s: e1T[j][:].bitcast(F32)[:, P * s:P * (s + 1)], finish)
 
         def run(steps):
             for fn, s in steps:
@@ -321,7 +320,8 @@ def tile_coattention_pa_kernel(tc, q, k, x1, x2, mask, Wv, bv, out_0, out_1):
             flush()
 
             def e1_exp(j):
-                nc.scalar.activation(out=e1T[j][:], in_=aT[j][:], func=ACT.Exp, bias=ncm[:, j:j + 1], scale=SCALE,
+                nc.scalar.activation(out=e1T[j][:].rearrange("p (v r e) -> p v r e", v=4, e=2),
+                                     in_=aT[j][:].rearrange("p (v e r) -> p v r e", v=4, e=2), func=ACT.Exp, bias=ncm[:, j:j + 1], scale=SCALE,
                                      accum_out=csum[:, j:j + 1])
 
             for j in range(4):

@@ -29,17 +29,12 @@ def tile_coattention_pa_kernel(tc, q, k, x1, x2, mask, Wv, bv, out_0, out_1):
 
         ident_f = const.tile([P, P], F32, name="ident_f")
         make_identity(nc, ident_f[:])
-        ones = const.tile([P, P], BF16, name="ones")
-        nc.vector.memset(ones[:], 1.0)
-        rows = const.tile([P, 1024], BF16, name="rows")
-        nc.vector.memset(rows[:], 0.0)
         warm = const.tile([P, 2], F32, name="warm")
         nc.vector.memset(warm[:], 0.0)
         nc.scalar.activation(out=warm[:, 1:2], in_=warm[:, 0:1], func=ACT.Exp)
         mcol_b = const.tile([P, 4], BF16, name="mcol_b")
         nc.scalar.dma_start(out=mcol_b[:], in_=mask.rearrange("b (r j) -> (b r) j", j=4))
-        nc.scalar.dma_start(out=rows[0:1, :], in_=bv.rearrange("(o n) -> o n", o=1))
-        bias_bc = const.tile([P, 1024], F32, name="bias_bc")
+        bias_bc = const.tile([P, 1024], BF16, name="bias_bc")
         mcol = const.tile([P, 4], F32, name="mcol")
         mterm = const.tile([P, 4], F32, name="mterm")
         cmx = const.tile([P, 8], F32, name="cmx")
@@ -57,7 +52,6 @@ def tile_coattention_pa_kernel(tc, q, k, x1, x2, mask, Wv, bv, out_0, out_1):
         o1_d = out_1.rearrange("b (r j) d -> (b r) j d", j=4)
 
         aT = [keep.tile([P, 1024], F32, name="aT%d" % j) for j in range(4)]
-        rm = [keep.tile([P, 512], F32, name="rm%d" % h) for h in range(2)]
         e2 = [keep.tile([P, 512], BF16, name="e2_%d" % i) for i in range(8)]
         e1T = [keep.tile([P, 1024], BF16, name="e1T%d" % j) for j in range(4)]
         x1c = [keep.tile([P, 256], U32, name="x1c%d" % i, align_bytes=64) for i in range(8)]
@@ -75,14 +69,25 @@ def tile_coattention_pa_kernel(tc, q, k, x1, x2, mask, Wv, bv, out_0, out_1):
         v2c = keep.tile([P, 1024], U32, name="v2c", align_bytes=64)
         v2s = keep.tile([P, 1024], U8, name="v2s", align_bytes=64)
 
-        waiting = []
-        issued = [0]
+        late = []
+
+        def after(n, fn):
+            late.append([n, fn])
+
+        def tick():
+            due = [item for item in late if item[0] <= 1]
+            rest = [[item[0] - 1, item[1]] for item in late if item[0] > 1]
+            late.clear()
+            late.extend(rest)
+            for item in due:
+                item[1]()
 
         def flush():
-            for n in range(issued[0], len(waiting)):
-                codes, scales, src = waiting[n]
-                nc.vector.quantize_mx(out=codes.bitcast(FP8X4), scales=scales, in_=src)
-            issued[0] = len(waiting)
+            for n in range(8):
+                tick()
+
+        def quantise(codes, scales, src):
+            nc.vector.quantize_mx(out=codes.bitcast(FP8X4), scales=scales, in_=src)
 
         def copy_on(eng, out, in_):
             if eng == "s":
@@ -101,20 +106,20 @@ def tile_coattention_pa_kernel(tc, q, k, x1, x2, mask, Wv, bv, out_0, out_1):
                     finish(box[0])
             return [(step, s) for s in range(count)]
 
-        def rm_job(h):
-            def finish(bank):
-                nc.vector.tensor_reduce(out=rmx[:, 4 * h:4 * h + 4], in_=bank[:].rearrange("p (i r) -> p i r", i=4),
-                                        axis=AX.X, op=ALU.max)
-                nc.vector.tensor_scalar_mul(out=nrm[:, 4 * h:4 * h + 4], in0=rmx[:, 4 * h:4 * h + 4], scalar1=-SCALE)
-            return job(4, F32, ident_f, lambda s: rm[h][:, P * s:P * (s + 1)], finish)
-
         def a_job(i):
             def finish(bank):
                 nc.vector.tensor_reduce(out=rmx[:, i:i + 1], in_=bank[:], axis=AX.X, op=ALU.max)
+                tick()
                 nc.vector.tensor_scalar_mul(out=nrm[:, i:i + 1], in0=rmx[:, i:i + 1], scalar1=-SCALE)
-                nc.scalar.activation(out=e2[i][:].rearrange("p (u r e) -> p u r e", u=2, e=2),
-                                     in_=bank[:].rearrange("p (u e r) -> p u r e", u=2, e=2), func=ACT.Exp,
-                                     bias=nrm[:, i:i + 1], scale=SCALE, accum_out=rsum[:, i:i + 1])
+
+                def exponentials():
+                    nc.scalar.activation(out=e2[i][:].rearrange("p (u r e) -> p u r e", u=2, e=2),
+                                         in_=bank[:].rearrange("p (u e r) -> p u r e", u=2, e=2), func=ACT.Exp,
+                                         bias=nrm[:, i:i + 1], scale=SCALE, accum_out=rsum[:, i:i + 1])
+                    if i % 2 == 1:
+                        nc.vector.reciprocal(out=rrs[:, i - 1:i + 1], in_=rsum[:, i - 1:i + 1])
+
+                after(2, exponentials)
             return job(4, F32, ident_f, lambda s: aT[s][:, P * i:P * (i + 1)], finish)
 
         def e2_job(pr, eng):
@@ -122,9 +127,8 @@ def tile_coattention_pa_kernel(tc, q, k, x1, x2, mask, Wv, bv, out_0, out_1):
                 eg = egp.tile([P, 1024], BF16, tag="eg", name="eg", align_bytes=64)
                 copy_on(eng, eg[:].bitcast(F32).rearrange("p (a c u) -> p a c u", a=2, u=2),
                         bank[:].rearrange("p (a u c) -> p a c u", a=2, u=2))
-                flush()
-                nc.vector.reciprocal(out=rrs[:, 2 * pr:2 * pr + 2], in_=rsum[:, 2 * pr:2 * pr + 2])
-                waiting.append((e2c[pr][:], e2s[pr][:], eg[:]))
+                tick()
+                after(1, lambda: quantise(e2c[pr][:], e2s[pr][:], eg[:]))
             return job(4, F32, ident_f, lambda s: e2[2 * pr + s // 2][:].bitcast(F32)[:, P * (s % 2):P * (s % 2 + 1)], finish)
 
         def e1_job(j, eng):
@@ -132,8 +136,8 @@ def tile_coattention_pa_kernel(tc, q, k, x1, x2, mask, Wv, bv, out_0, out_1):
                 eg = egp.tile([P, 1024], BF16, tag="eg", name="eg", align_bytes=64)
                 copy_on(eng, eg[:].bitcast(F32).rearrange("p (g c u) -> p g c u", g=2, u=2),
                         bank[:].rearrange("p (g u c) -> p g c u", g=2, u=2))
-                flush()
-                waiting.append((e1c[j][:], e1s[j][:], eg[:]))
+                tick()
+                after(1, lambda: quantise(e1c[j][:], e1s[j][:], eg[:]))
             return job(4, F32, ident_f, lambda s: e1T[j][:].bitcast(F32)[:, P * s:P * (s + 1)], finish)
 
         def run(steps):
@@ -162,14 +166,15 @@ def tile_coattention_pa_kernel(tc, q, k, x1, x2, mask, Wv, bv, out_0, out_1):
                                     in0=acc[:].rearrange("p (t w) -> p w t", t=4),
                                     in1=bias_bc[:, P * c:P * (c + 1)].unsqueeze(2).to_broadcast([P, P, 4]),
                                     op=ALU.add)
-            flush()
+            tick()
 
         def v_half(xc, xs, base, h, codes, scales, between):
             vg = vgp.tile([P, 2048], BF16, tag="vg", name="vg", align_bytes=64)
             for cc in range(4):
                 v_bank(xc, xs, base, 4 * h + cc, vg)
+                if cc == 3:
+                    after(1, lambda: quantise(codes[:, 512 * h:512 * (h + 1)], scales[:, 512 * h:512 * (h + 1)], vg[:]))
                 between(cc)
-            waiting.append((codes[:, 512 * h:512 * (h + 1)], scales[:, 512 * h:512 * (h + 1)], vg[:]))
 
         def scale_out(eng, acc, sc, dst):
             o = ost.tile([P, 512], F32, tag="o", name="o")
@@ -177,6 +182,7 @@ def tile_coattention_pa_kernel(tc, q, k, x1, x2, mask, Wv, bv, out_0, out_1):
                 nc.scalar.activation(out=o[:], in_=acc[:], func=ACT.Copy, scale=sc)
             else:
                 nc.vector.tensor_scalar_mul(out=o[:], in0=acc[:], scalar1=sc)
+            tick()
             nc.sync.dma_start(out=dst, in_=o[:])
 
         def x2o(i, h, eng):
@@ -231,6 +237,8 @@ def tile_coattention_pa_kernel(tc, q, k, x1, x2, mask, Wv, bv, out_0, out_1):
             for c in range(0, 8, 2):
                 load_two(w_raw[c // 4], c % 4, w_d[:, c:c + 2, :])
             for i in range(0, 8, 2):
+                if i == 4:
+                    nc.sync.dma_start(out=bias_bc[:], in_=bv.partition_broadcast(P))
                 load_two(x1_raw[i // 4], i % 4, x1_d[i // 4][:, i % 4:i % 4 + 2, :])
 
             kT = [raw.tile([P, 512], F32, name="kT%d" % j) for j in range(4)]
@@ -256,8 +264,8 @@ def tile_coattention_pa_kernel(tc, q, k, x1, x2, mask, Wv, bv, out_0, out_1):
                     xg = xgp.tile([P, 1024], BF16, tag="xg", name="xg", align_bytes=64)
                     copy_on(eng, xg[:].bitcast(F32).rearrange("p (g r u) -> p g r u", g=2, u=2),
                             bank[:].rearrange("p (g u r) -> p g r u", g=2, u=2))
-                    flush()
-                    waiting.append((codes[:], scales[:], xg[:]))
+                    tick()
+                    after(1, lambda: quantise(codes[:], scales[:], xg[:]))
                 return job(4, F32, ident_f, words_of(raw_tile, t), finish)
 
             def leave_scores(acc, j, h):
@@ -287,26 +295,26 @@ def tile_coattention_pa_kernel(tc, q, k, x1, x2, mask, Wv, bv, out_0, out_1):
             for j in range(2, 4):
                 queue.extend(k_job(j, "s"))
             for i in range(4, 8):
-                queue.extend(q_job(i, "ss"[i % 2]))
+                queue.extend(q_job(i, "s"))
             for i in range(4):
-                queue.extend(mx_job(x2_raw, i, x2c[i], x2s[i], "ssss"[i % 4]))
+                queue.extend(mx_job(x2_raw, i, x2c[i], x2s[i], "s"))
             for c in range(8):
-                queue.extend(mx_job(w_raw[c // 4], c % 4, wc[c], ws[c], "ssss"[c % 4]))
+                queue.extend(mx_job(w_raw[c // 4], c % 4, wc[c], ws[c], "s"))
             for h in range(2):
                 for j in range(4):
                     if (j, h) == (0, 0):
                         continue
-                    if (j, h) == (1, 0):
-                        for hh in range(2):
-                            b_ps = ps.tile([P, 512], F32, tag="b", name="b_ps")
-                            nc.tensor.matmul(b_ps[:], lhsT=ones[:], rhs=rows[:, 512 * hh:512 * (hh + 1)], start=True, stop=True)
-                            weave(2)
-                            nc.vector.tensor_copy(out=bias_bc[:, 512 * hh:512 * (hh + 1)], in_=b_ps[:])
                     if (j, h) == (1, 1):
-                        queue[taken[0]:taken[0]] = (a_job(0) + a_job(1) + a_job(2) + a_job(3)
-                                                    + e2_job(0, "s") + e2_job(1, "s"))
                         for i in range(8):
-                            queue.extend(mx_job(x1_raw[i // 4], i % 4, x1c[i], x1s[i], "ssss"[i % 4]))
+                            queue.extend(mx_job(x1_raw[i // 4], i % 4, x1c[i], x1s[i], "s"))
+                        at = taken[0]
+                        for steps in (a_job(0), a_job(1), a_job(2), a_job(3)):
+                            queue[at:at] = steps
+                            at += 8
+                        for steps in (e2_job(0, "s"), e2_job(1, "s")):
+                            at += 4
+                            queue[at:at] = steps
+                            at += 4
                     acc = ps.tile([P, 512], F32, tag="b", name="acc")
                     for n in range(8):
                         score_pass(acc, j, h, slice(0, 512), n)
@@ -316,35 +324,38 @@ def tile_coattention_pa_kernel(tc, q, k, x1, x2, mask, Wv, bv, out_0, out_1):
             weave(len(queue))
             nc.vector.tensor_reduce(out=cm4[:], in_=cmx[:].rearrange("p (h j) -> p j h", h=2), axis=AX.X, op=ALU.max)
             nc.vector.tensor_scalar_mul(out=ncm[:], in0=cm4[:], scalar1=-SCALE)
-            run(a_job(4) + a_job(5) + a_job(6) + a_job(7))
-            flush()
-
             def e1_exp(j):
                 nc.scalar.activation(out=e1T[j][:].rearrange("p (v r e) -> p v r e", v=4, e=2),
-                                     in_=aT[j][:].rearrange("p (v e r) -> p v r e", v=4, e=2), func=ACT.Exp, bias=ncm[:, j:j + 1], scale=SCALE,
-                                     accum_out=csum[:, j:j + 1])
+                                     in_=aT[j][:].rearrange("p (v e r) -> p v r e", v=4, e=2), func=ACT.Exp,
+                                     bias=ncm[:, j:j + 1], scale=SCALE, accum_out=csum[:, j:j + 1])
 
-            for j in range(4):
-                e1_exp(j)
+            run(a_job(4) + a_job(5) + a_job(6) + a_job(7))
             for h in range(2):
                 v_half(x2c, x2s, 0, h, v2c, v2s, lambda cc: None)
-            run(e2_job(2, "s") + e2_job(3, "v"))
+                e1_exp(2 * h)
+                e1_exp(2 * h + 1)
+            run(e2_job(2, "s") + e2_job(3, "s"))
 
         ost = ctx.enter_context(tc.tile_pool(name="ost", bufs=16))
 
-        def two_x2o(first, cc):
-            for i in range(2):
-                x2o(first + 2 * (cc % 2) + i, cc // 2, "ss"[(2 * cc + i) % 2])
+        outs = [(i, h) for h in range(2) for i in range(4)] + [(i, h) for h in range(2) for i in range(4, 8)]
 
-        v_half(x1c, x1s, 0, 0, v1c[0], v1s[0], lambda cc: two_x2o(0, cc))
+        sent = [0]
+
+        def some_x2o(n):
+            for i, h in outs[sent[0]:sent[0] + n]:
+                x2o(i, h, "s")
+            sent[0] += n
+
+        v_half(x1c, x1s, 0, 0, v1c[0], v1s[0], lambda cc: some_x2o(1 + cc % 2))
         run(e1_job(0, "s") + e1_job(1, "v") + e1_job(2, "s") + e1_job(3, "v"))
         nc.vector.reciprocal(out=crec[:], in_=csum[:])
         nc.vector.tensor_mul(rc[:], crec[:], mcol[:])
-        v_half(x1c, x1s, 4, 0, v1c[1], v1s[1], lambda cc: two_x2o(4, cc))
-        v_half(x1c, x1s, 0, 1, v1c[0], v1s[0], lambda cc: None)
+        v_half(x1c, x1s, 4, 0, v1c[1], v1s[1], lambda cc: some_x2o(1 + cc % 2))
+        v_half(x1c, x1s, 0, 1, v1c[0], v1s[0], lambda cc: some_x2o(1))
         v_half(x1c, x1s, 4, 1, v1c[1], v1s[1], lambda cc: x1m(cc // 2, 0, "s") if cc % 2 == 1 else None)
-        for j in range(2, 4):
-            x1m(j, 0, "sv"[j % 2])
-            flush()
+        x1m(2, 0, "s")
+        x1m(3, 0, "v")
+        flush()
         for j in range(4):
             x1m(j, 1, "sv"[j % 2])

@@ -29,6 +29,8 @@ def tile_coattention_pa_kernel(tc, q, k, x1, x2, mask, Wv, bv, out_0, out_1):
 
         ident_f = const.tile([P, P], F32, name="ident_f")
         make_identity(nc, ident_f[:])
+        zero = const.tile([P, 512], BF16, name="zero")
+        nc.vector.memset(zero[:], 0.0)
         warm = const.tile([P, 2], F32, name="warm")
         nc.vector.memset(warm[:], 0.0)
         nc.scalar.activation(out=warm[:, 1:2], in_=warm[:, 0:1], func=ACT.Exp)
@@ -277,14 +279,18 @@ def tile_coattention_pa_kernel(tc, q, k, x1, x2, mask, Wv, bv, out_0, out_1):
                 nc.tensor.matmul(acc[:, cols], lhsT=kT_b[j][:, n // 2, :, n % 2], rhs=qT_b[h][:, n // 2, cols, n % 2],
                                  start=(n == 0), stop=(n == 7))
 
+            heat = ps.tile([P, 512], F32, tag="b", name="heat")
+            for n in range(5):
+                nc.tensor.matmul(heat[:], lhsT=zero[:, 0:P], rhs=zero[:], start=True, stop=True)
+
+            ahead = [q_job(2, "v"), q_job(3, "s"), k_job(1, "v")]
             run(k_job(0, "s"))
             run(q_job(0, "v"))
+            run(q_job(1, "s"))
             acc = ps.tile([P, 512], F32, tag="b", name="acc")
             for i in range(4):
                 if i < 3:
-                    run(q_job(i + 1, "sv"[i % 2]))
-                else:
-                    run(k_job(1, "s"))
+                    run(ahead[i])
                 for n in range(8):
                     score_pass(acc, 0, 0, slice(P * i, P * (i + 1)), n)
             nc.vector.tensor_copy(out=mcol[:], in_=mcol_b[:])

@@ -239,9 +239,8 @@ def tile_coattention_pa_kernel(tc, q, k, x1, x2, mask, Wv, bv, out_0, out_1):
             for c in range(0, 8, 2):
                 load_two(w_raw[c // 4], c % 4, w_d[:, c:c + 2, :])
             for i in range(0, 8, 2):
-                if i == 4:
-                    nc.sync.dma_start(out=bias_bc[:], in_=bv.partition_broadcast(P))
                 load_two(x1_raw[i // 4], i % 4, x1_d[i // 4][:, i % 4:i % 4 + 2, :])
+            nc.sync.dma_start(out=bias_bc[:], in_=bv.partition_broadcast(P))
 
             kT = [raw.tile([P, 512], F32, name="kT%d" % j) for j in range(4)]
             kT_b = [t[:].bitcast(BF16).rearrange("p (u r e) -> p u r e", u=4, e=2) for t in kT]

@@ -130,7 +130,7 @@ def tile_coattention_pa_kernel(tc, q, k, x1, x2, mask, Wv, bv, out_0, out_1):
                 copy_on(eng, eg[:].bitcast(F32).rearrange("p (a c u) -> p a c u", a=2, u=2),
                         bank[:].rearrange("p (a u c) -> p a c u", a=2, u=2))
                 tick()
-                after(1, lambda: quantise(e2c[pr][:], e2s[pr][:], eg[:]))
+                after(3, lambda: quantise(e2c[pr][:], e2s[pr][:], eg[:]))
             return job(4, F32, ident_f, lambda s: e2[2 * pr + s // 2][:].bitcast(F32)[:, P * (s % 2):P * (s % 2 + 1)], finish)
 
         def e1_job(j, eng):
@@ -139,7 +139,7 @@ def tile_coattention_pa_kernel(tc, q, k, x1, x2, mask, Wv, bv, out_0, out_1):
                 copy_on(eng, eg[:].bitcast(F32).rearrange("p (g c u) -> p g c u", g=2, u=2),
                         bank[:].rearrange("p (g u c) -> p g c u", g=2, u=2))
                 tick()
-                after(1, lambda: quantise(e1c[j][:], e1s[j][:], eg[:]))
+                after(3, lambda: quantise(e1c[j][:], e1s[j][:], eg[:]))
             return job(4, F32, ident_f, lambda s: e1T[j][:].bitcast(F32)[:, P * s:P * (s + 1)], finish)
 
         def run(steps):
@@ -266,7 +266,7 @@ def tile_coattention_pa_kernel(tc, q, k, x1, x2, mask, Wv, bv, out_0, out_1):
                     copy_on(eng, xg[:].bitcast(F32).rearrange("p (g r u) -> p g r u", g=2, u=2),
                             bank[:].rearrange("p (g u r) -> p g r u", g=2, u=2))
                     tick()
-                    after(1, lambda: quantise(codes[:], scales[:], xg[:]))
+                    after(3, lambda: quantise(codes[:], scales[:], xg[:]))
                 return job(4, F32, ident_f, words_of(raw_tile, t), finish)
 
             def leave_scores(acc, j, h):

from contextlib import ExitStack

import concourse.mybir as mybir
from concourse.masks import make_identity

F32 = mybir.dt.float32
BF16 = mybir.dt.bfloat16
U32 = mybir.dt.uint32
U8 = mybir.dt.uint8
FP8X4 = mybir.dt.float8_e4m3fn_x4
ALU = mybir.AluOpType
ACT = mybir.ActivationFunctionType
AX = mybir.AxisListType

P = 128
FLOPS = 2 * (1024 + 512) * 1024 * 1024 + 3 * 2 * 1024 * 512 * 1024
SCALE = 0.03125


def tile_coattention_pa_kernel(tc, q, k, x1, x2, mask, Wv, bv, out_0, out_1):
    nc = tc.nc
    with ExitStack() as ctx:
        ctx.enter_context(tc.manual_schedule())
        const = ctx.enter_context(tc.tile_pool(name="const", bufs=1))
        keep = ctx.enter_context(tc.tile_pool(name="keep", bufs=1))
        egp = ctx.enter_context(tc.tile_pool(name="egp", bufs=4))
        vgp = ctx.enter_context(tc.tile_pool(name="vgp", bufs=3))
        ps = ctx.enter_context(tc.psum_pool(name="ps", bufs=8))

        ident_f = const.tile([P, P], F32, name="ident_f")
        make_identity(nc, ident_f[:])
        zero = const.tile([P, 512], BF16, name="zero")
        nc.vector.memset(zero[:], 0.0)
        warm = const.tile([P, 2], F32, name="warm")
        nc.vector.memset(warm[:], 0.0)
        nc.scalar.activation(out=warm[:, 1:2], in_=warm[:, 0:1], func=ACT.Exp)
        mcol_b = const.tile([P, 4], BF16, name="mcol_b")
        nc.scalar.dma_start(out=mcol_b[:], in_=mask.rearrange("b (r j) -> (b r) j", j=4))
        bias_bc = const.tile([P, 1024], BF16, name="bias_bc")
        mcol = const.tile([P, 4], F32, name="mcol")
        mterm = const.tile([P, 4], F32, name="mterm")
        cmx = const.tile([P, 8], F32, name="cmx")
        cm4 = const.tile([P, 4], F32, name="cm4")
        ncm = const.tile([P, 4], F32, name="ncm")
        csum = const.tile([P, 4], F32, name="csum")
        crec = const.tile([P, 4], F32, name="crec")
        rc = const.tile([P, 4], F32, name="rc")
        rmx = const.tile([P, 8], F32, name="rmx")
        nrm = const.tile([P, 8], F32, name="nrm")
        rsum = const.tile([P, 8], F32, name="rsum")
        rrs = const.tile([P, 8], F32, name="rrs")

        o0_d = out_0.rearrange("b (g p t) d -> (b g) p t d", g=2, t=4)
        o1_d = out_1.rearrange("b (r j) d -> (b r) j d", j=4)

        aT = [keep.tile([P, 1024], F32, name="aT%d" % j) for j in range(4)]
        e2 = [keep.tile([P, 512], BF16, name="e2_%d" % i) for i in range(8)]
        e1T = [keep.tile([P, 1024], BF16, name="e1T%d" % j) for j in range(4)]
        x1c = [keep.tile([P, 256], U32, name="x1c%d" % i, align_bytes=64) for i in range(8)]
        x1s = [keep.tile([P, 256], U8, name="x1s%d" % i, align_bytes=64) for i in range(8)]
        x2c = [keep.tile([P, 256], U32, name="x2c%d" % i, align_bytes=64) for i in range(4)]
        x2s = [keep.tile([P, 256], U8, name="x2s%d" % i, align_bytes=64) for i in range(4)]
        wc = [keep.tile([P, 256], U32, name="wc%d" % i, align_bytes=64) for i in range(8)]
        ws = [keep.tile([P, 256], U8, name="ws%d" % i, align_bytes=64) for i in range(8)]
        e2c = [keep.tile([P, 256], U32, name="e2c%d" % i, align_bytes=64) for i in range(4)]
        e2s = [keep.tile([P, 256], U8, name="e2s%d" % i, align_bytes=64) for i in range(4)]
        e1c = [keep.tile([P, 256], U32, name="e1c%d" % i, align_bytes=64) for i in range(4)]
        e1s = [keep.tile([P, 256], U8, name="e1s%d" % i, align_bytes=64) for i in range(4)]
        v1c = [keep.tile([P, 1024], U32, name="v1c%d" % i, align_bytes=64) for i in range(2)]
        v1s = [keep.tile([P, 1024], U8, name="v1s%d" % i, align_bytes=64) for i in range(2)]
        v2c = keep.tile([P, 1024], U32, name="v2c", align_bytes=64)
        v2s = keep.tile([P, 1024], U8, name="v2s", align_bytes=64)

        late = []

        def after(n, fn):
            late.append([n, fn])

        def tick():
            due = [item for item in late if item[0] <= 1]
            rest = [[item[0] - 1, item[1]] for item in late if item[0] > 1]
            late.clear()
            late.extend(rest)
            for item in due:
                item[1]()

        def flush():
            for n in range(8):
                tick()

        def quantise(codes, scales, src):
            nc.vector.quantize_mx(out=codes.bitcast(FP8X4), scales=scales, in_=src)

        def copy_on(eng, out, in_):
            if eng == "s":
                nc.scalar.copy(out=out, in_=in_)
            else:
                nc.vector.tensor_copy(out=out, in_=in_)

        def job(count, dtype, ident, src_of, finish):
            box = []

            def step(s):
                if s == 0:
                    box.append(ps.tile([P, count * P], dtype, tag="b", name="bank"))
                nc.tensor.transpose(box[0][:, P * s:P * (s + 1)], src_of(s), ident[:])
                if s == count - 1:
                    finish(box[0])
            return [(step, s) for s in range(count)]

        def a_job(i):
            def finish(bank):
                nc.vector.tensor_reduce(out=rmx[:, i:i + 1], in_=bank[:], axis=AX.X, op=ALU.max)
                tick()
                nc.vector.tensor_scalar_mul(out=nrm[:, i:i + 1], in0=rmx[:, i:i + 1], scalar1=-SCALE)

                def exponentials():
                    nc.scalar.activation(out=e2[i][:].rearrange("p (u r e) -> p u r e", u=2, e=2),
                                         in_=bank[:].rearrange("p (u e r) -> p u r e", u=2, e=2), func=ACT.Exp,
                                         bias=nrm[:, i:i + 1], scale=SCALE, accum_out=rsum[:, i:i + 1])
                    if i % 2 == 1:
                        nc.vector.reciprocal(out=rrs[:, i - 1:i + 1], in_=rsum[:, i - 1:i + 1])

                after(2, exponentials)
            return job(4, F32, ident_f, lambda s: aT[s][:, P * i:P * (i + 1)], finish)

        def e2_job(pr, eng):
            def finish(bank):
                eg = egp.tile([P, 1024], BF16, tag="eg", name="eg", align_bytes=64)
                copy_on(eng, eg[:].bitcast(F32).rearrange("p (a c u) -> p a c u", a=2, u=2),
                        bank[:].rearrange("p (a u c) -> p a c u", a=2, u=2))
                tick()
                after(3, lambda: quantise(e2c[pr][:], e2s[pr][:], eg[:]))
            return job(4, F32, ident_f, lambda s: e2[2 * pr + s // 2][:].bitcast(F32)[:, P * (s % 2):P * (s % 2 + 1)], finish)

        def e1_job(j, eng):
            def finish(bank):
                eg = egp.tile([P, 1024], BF16, tag="eg", name="eg", align_bytes=64)
                copy_on(eng, eg[:].bitcast(F32).rearrange("p (g c u) -> p g c u", g=2, u=2),
                        bank[:].rearrange("p (g u c) -> p g c u", g=2, u=2))
                tick()
                after(3, lambda: quantise(e1c[j][:], e1s[j][:], eg[:]))
            return job(4, F32, ident_f, lambda s: e1T[j][:].bitcast(F32)[:, P * s:P * (s + 1)], finish)

        def run(steps):
            for fn, s in steps:
                fn(s)

        queue = []
        taken = [0]

        def weave(n):
            run(queue[taken[0]:taken[0] + n])
            taken[0] = min(taken[0] + n, len(queue))

        def v_bank(xc, xs, base, c, vg):
            acc = ps.tile([P, 512], F32, tag="b", name="v_ps")
            for t in range(4):
                for g in range(2):
                    nc.tensor.matmul_mx(out=acc[:, P * t:P * (t + 1)],
                                        lhsT=xc[base + t][:, P * g:P * (g + 1)].bitcast(FP8X4),
                                        lhsT_scale=xs[base + t][:, P * g:P * (g + 1)],
                                        rhs=wc[c][:, P * g:P * (g + 1)].bitcast(FP8X4),
                                        rhs_scale=ws[c][:, P * g:P * (g + 1)],
                                        start=(g == 0), stop=(g == 1))
            cc = c % 4
            nc.vector.tensor_tensor(out=vg[:].rearrange("p (w t) -> p w t", t=4)[:, P * cc:P * (cc + 1), :],
                                    in0=acc[:].rearrange("p (t w) -> p w t", t=4),
                                    in1=bias_bc[:, P * c:P * (c + 1)].unsqueeze(2).to_broadcast([P, P, 4]),
                                    op=ALU.add)
            tick()

        def v_half(xc, xs, base, h, codes, scales, between):
            vg = vgp.tile([P, 2048], BF16, tag="vg", name="vg", align_bytes=64)
            for cc in range(4):
                v_bank(xc, xs, base, 4 * h + cc, vg)
                if cc == 3:
                    after(1, lambda: quantise(codes[:, 512 * h:512 * (h + 1)], scales[:, 512 * h:512 * (h + 1)], vg[:]))
                between(cc)

        def scale_out(eng, acc, sc, dst):
            o = ost.tile([P, 512], F32, tag="o", name="o")
            if eng == "s":
                nc.scalar.activation(out=o[:], in_=acc[:], func=ACT.Copy, scale=sc)
            else:
                nc.vector.tensor_scalar_mul(out=o[:], in0=acc[:], scalar1=sc)
            tick()
            nc.sync.dma_start(out=dst, in_=o[:])

        def x2o(i, h, eng):
            acc = ps.tile([P, 512], F32, tag="b", name="o2_ps")
            pr, ii = i // 2, i % 2
            nc.tensor.matmul_mx(out=acc[:], lhsT=e2c[pr][:, P * ii:P * (ii + 1)].bitcast(FP8X4),
                                lhsT_scale=e2s[pr][:, P * ii:P * (ii + 1)],
                                rhs=v2c[:, 512 * h:512 * (h + 1)].bitcast(FP8X4),
                                rhs_scale=v2s[:, 512 * h:512 * (h + 1)], start=True, stop=True)
            scale_out(eng, acc, rrs[:, i:i + 1], o0_d[i // 4][:, i % 4, 512 * h:512 * (h + 1)])

        def x1m(j, h, eng):
            acc = ps.tile([P, 512], F32, tag="b", name="o1_ps")
            for g in range(2):
                nc.tensor.matmul_mx(out=acc[:], lhsT=e1c[j][:, P * g:P * (g + 1)].bitcast(FP8X4),
                                    lhsT_scale=e1s[j][:, P * g:P * (g + 1)],
                                    rhs=v1c[g][:, 512 * h:512 * (h + 1)].bitcast(FP8X4),
                                    rhs_scale=v1s[g][:, 512 * h:512 * (h + 1)], start=(g == 0), stop=(g == 1))
            scale_out(eng, acc, rc[:, j:j + 1], o1_d[:, j, 512 * h:512 * (h + 1)])


        with ExitStack() as early:
            xgp = early.enter_context(tc.tile_pool(name="xgp", bufs=6))
            raw = early.enter_context(tc.tile_pool(name="raw", bufs=1))
            k_raw = raw.tile([P, 4096], BF16, name="k_raw")
            q_raw = [raw.tile([P, 4096], BF16, name="q_raw%d" % g) for g in range(2)]
            x2_raw = raw.tile([P, 4096], BF16, name="x2_raw")
            w_raw = [raw.tile([P, 4096], BF16, name="w_raw%d" % g) for g in range(2)]
            x1_raw = [raw.tile([P, 4096], BF16, name="x1_raw%d" % g) for g in range(2)]
            k_d = k.rearrange("b (p t) d -> (b p) t d", t=4)
            q_d = q.rearrange("b (g p t) d -> (b g) p t d", g=2, t=4)
            x2_d = x2.rearrange("b (p t) d -> (b p) t d", t=4)
            x1_d = x1.rearrange("b (g p t) d -> (b g) p t d", g=2, t=4)
            w_d = Wv.rearrange("(c p) d -> p c d", p=P)

            def load(dst, t, src):
                nc.sync.dma_start(out=dst[:, 1024 * t:1024 * (t + 1)], in_=src)

            load(k_raw, 0, k_d[:, 0, :])
            for t in range(4):
                load(q_raw[0], t, q_d[0][:, t, :])
            for t in range(1, 4):
                load(k_raw, t, k_d[:, t, :])
            for t in range(4):
                load(q_raw[1], t, q_d[1][:, t, :])

            def load_two(dst, t, src):
                nc.sync.dma_start(out=dst[:, 1024 * t:1024 * (t + 2)].rearrange("p (t d) -> p t d", t=2), in_=src)

            for t in range(0, 4, 2):
                load_two(x2_raw, t, x2_d[:, t:t + 2, :])
            for c in range(0, 8, 2):
                load_two(w_raw[c // 4], c % 4, w_d[:, c:c + 2, :])
            for i in range(0, 8, 2):
                load_two(x1_raw[i // 4], i % 4, x1_d[i // 4][:, i % 4:i % 4 + 2, :])
            nc.sync.dma_start(out=bias_bc[:], in_=bv.partition_broadcast(P))

            kT = [raw.tile([P, 512], F32, name="kT%d" % j) for j in range(4)]
            kT_b = [t[:].bitcast(BF16).rearrange("p (u r e) -> p u r e", u=4, e=2) for t in kT]
            qT = [raw.tile([P, 2048], F32, name="qT%d" % h) for h in range(2)]
            qT_w = [t[:].rearrange("p (u c) -> p u c", u=4) for t in qT]
            qT_b = [t[:].bitcast(BF16).rearrange("p (u c e) -> p u c e", u=4, e=2) for t in qT]

            def words_of(raw_tile, t):
                words = raw_tile[:].bitcast(F32)
                return lambda s: words[:, 512 * t + P * s:512 * t + P * (s + 1)]

            def k_job(j, eng):
                return job(4, F32, ident_f, words_of(k_raw, j), lambda bank: copy_on(eng, kT[j][:], bank[:]))

            def q_job(i, eng):
                return job(4, F32, ident_f, words_of(q_raw[i // 4], i % 4),
                           lambda bank: copy_on(eng, qT_w[i // 4][:, :, P * (i % 4):P * (i % 4 + 1)],
                                                bank[:].rearrange("p (u r) -> p u r", u=4)))

            def mx_job(raw_tile, t, codes, scales, eng):
                def finish(bank):
                    xg = xgp.tile([P, 1024], BF16, tag="xg", name="xg", align_bytes=64)
                    copy_on(eng, xg[:].bitcast(F32).rearrange("p (g r u) -> p g r u", g=2, u=2),
                            bank[:].rearrange("p (g u r) -> p g r u", g=2, u=2))
                    tick()
                    after(3, lambda: quantise(codes[:], scales[:], xg[:]))
                return job(4, F32, ident_f, words_of(raw_tile, t), finish)

            def leave_scores(acc, j, h):
                half = aT[j][:, 512 * h:512 * (h + 1)]
                nc.vector.tensor_scalar(out=half, in0=acc[:], scalar1=mterm[:, j:j + 1], scalar2=None, op0=ALU.add,
                                        op1=ALU.max, accum_out=cmx[:, 4 * h + j:4 * h + j + 1])

            def score_pass(acc, j, h, cols, n):
                nc.tensor.matmul(acc[:, cols], lhsT=kT_b[j][:, n // 2, :, n % 2], rhs=qT_b[h][:, n // 2, cols, n % 2],
                                 start=(n == 0), stop=(n == 7))

            heat = ps.tile([P, 512], F32, tag="b", name="heat")
            for n in range(5):
                nc.tensor.matmul(heat[:], lhsT=zero[:, 0:P], rhs=zero[:], start=True, stop=True)

            ahead = [q_job(2, "v"), q_job(3, "s"), k_job(1, "v")]
            run(k_job(0, "s"))
            run(q_job(0, "v"))
            run(q_job(1, "s"))
            acc = ps.tile([P, 512], F32, tag="b", name="acc")
            for i in range(4):
                if i < 3:
                    run(ahead[i])
                for n in range(8):
                    score_pass(acc, 0, 0, slice(P * i, P * (i + 1)), n)
            nc.vector.tensor_copy(out=mcol[:], in_=mcol_b[:])
            nc.vector.tensor_scalar(out=mterm[:], in0=mcol[:], scalar1=1.0e30 / SCALE, scalar2=-1.0e30 / SCALE,
                                    op0=ALU.mult, op1=ALU.add)
            leave_scores(acc, 0, 0)

            for j in range(2, 4):
                queue.extend(k_job(j, "s"))
            for i in range(4, 8):
                queue.extend(q_job(i, "s"))
            for i in range(4):
                queue.extend(mx_job(x2_raw, i, x2c[i], x2s[i], "s"))
            for c in range(8):
                queue.extend(mx_job(w_raw[c // 4], c % 4, wc[c], ws[c], "s"))
            for h in range(2):
                for j in range(4):
                    if (j, h) == (0, 0):
                        continue
                    if (j, h) == (1, 1):
                        for i in range(8):
                            queue.extend(mx_job(x1_raw[i // 4], i % 4, x1c[i], x1s[i], "s"))
                        at = taken[0]
                        for steps in (a_job(0), a_job(1), a_job(2), a_job(3)):
                            queue[at:at] = steps
                            at += 8
                        for steps in (e2_job(0, "s"), e2_job(1, "s")):
                            at += 4
                            queue[at:at] = steps
                            at += 4
                    acc = ps.tile([P, 512], F32, tag="b", name="acc")
                    for n in range(8):
                        score_pass(acc, j, h, slice(0, 512), n)
                        weave(2)
                    leave_scores(acc, j, h)

            weave(len(queue))
            nc.vector.tensor_reduce(out=cm4[:], in_=cmx[:].rearrange("p (h j) -> p j h", h=2), axis=AX.X, op=ALU.max)
            nc.vector.tensor_scalar_mul(out=ncm[:], in0=cm4[:], scalar1=-SCALE)
            def e1_exp(j):
                nc.scalar.activation(out=e1T[j][:].rearrange("p (v r e) -> p v r e", v=4, e=2),
                                     in_=aT[j][:].rearrange("p (v e r) -> p v r e", v=4, e=2), func=ACT.Exp,
                                     bias=ncm[:, j:j + 1], scale=SCALE, accum_out=csum[:, j:j + 1])

            run(a_job(4) + a_job(5) + a_job(6) + a_job(7))
            for h in range(2):
                v_half(x2c, x2s, 0, h, v2c, v2s, lambda cc: None)
                e1_exp(2 * h)
                e1_exp(2 * h + 1)
            run(e2_job(2, "s") + e2_job(3, "s"))

        ost = ctx.enter_context(tc.tile_pool(name="ost", bufs=16))

        outs = [(i, h) for h in range(2) for i in range(4)] + [(i, h) for h in range(2) for i in range(4, 8)]

        sent = [0]

        def some_x2o(n):
            for i, h in outs[sent[0]:sent[0] + n]:
                x2o(i, h, "s")
            sent[0] += n

        v_half(x1c, x1s, 0, 0, v1c[0], v1s[0], lambda cc: some_x2o(1 + cc % 2))
        run(e1_job(0, "s") + e1_job(1, "v") + e1_job(2, "s") + e1_job(3, "v"))
        nc.vector.reciprocal(out=crec[:], in_=csum[:])
        nc.vector.tensor_mul(rc[:], crec[:], mcol[:])
        v_half(x1c, x1s, 4, 0, v1c[1], v1s[1], lambda cc: some_x2o(1 + cc % 2))
        v_half(x1c, x1s, 0, 1, v1c[0], v1s[0], lambda cc: some_x2o(1))
        v_half(x1c, x1s, 4, 1, v1c[1], v1s[1], lambda cc: x1m(cc // 2, 0, "s") if cc % 2 == 1 else None)
        x1m(2, 0, "s")
        x1m(3, 0, "v")
        flush()
        for j in range(4):
            x1m(j, 1, "sv"[j % 2])
